import numpy as np
import ml_dtypes


def mxq(x, axis, fmt="e4m3"):
    dtype, down = {"e4m3": (ml_dtypes.float8_e4m3fn, 7), "e5m2": (ml_dtypes.float8_e5m2, 14)}[fmt]
    v = np.moveaxis(np.asarray(x, np.float32).astype(ml_dtypes.bfloat16).astype(np.float64), axis, -1)
    blocks = v.reshape(v.shape[:-1] + (-1, 32))
    amax = np.abs(blocks).max(-1, keepdims=True)
    byte = np.maximum(np.where(amax > 0, np.frexp(amax)[1] - 1 + 127, 0) - down, 1)
    scale = np.exp2(byte - 127.0)
    codes = (blocks / scale).astype(np.float32).astype(dtype).astype(np.float64)
    return np.moveaxis((codes * scale).reshape(v.shape), -1, axis)


WIDE = False


def mx_kscale(k):
    if not WIDE:
        return np.ones(k)
    levels = np.array([10, -10, 5, -5, 0])
    a = np.random.permutation(np.resize(levels, k // 512 * 4)).reshape(k // 512, 4)
    idx = np.arange(k)
    return np.exp2(a[idx // 512, idx % 128 // 32])


BF16 = ml_dtypes.bfloat16


def bf(x):
    return np.asarray(x, np.float32).astype(BF16)


def f64(x):
    return np.asarray(x).astype(np.float64)


B, C, H, W, D, R = 2, 2048, 16, 16, 512, 3
P = R * R
CEN = P // 2
NB = P - 1
PAD = R // 2
KC = NB * C


def neighbours(z):
    zp = np.pad(z, ((0, 0), (0, 0), (PAD, PAD), (PAD, PAD)))
    views = [zp[:, :, di:di + H, dj:dj + W] for di in range(R) for dj in range(R) if di * R + dj != CEN]
    return np.stack(views, axis=2)


def setup_inputs():
    s = mx_kscale(KC)[::NB]
    t = mx_kscale(D)
    return {"z": bf(np.random.standard_normal((B, C, H, W)) * s[None, :, None, None]),
            "W1": bf((np.random.standard_normal((D, C, P)) / np.sqrt(KC) / s[None, :, None] * t[:, None, None]).reshape(D, C * P)),
            "b1": bf(np.random.standard_normal(D) * 0.3 * t),
            "W2": bf(np.random.standard_normal((C, D)) / np.sqrt(D) / t[None, :]),
            "b2": bf(np.random.standard_normal(C) * 0.3)}


def reference(z, W1, b1, W2, b2):
    win = neighbours(f64(z)).transpose(0, 3, 4, 1, 2).reshape(B * H * W, KC)
    w1 = np.delete(f64(W1).reshape(D, C, P), CEN, axis=2).reshape(D, KC)
    h = np.maximum((mxq(win, 1, "e4m3") @ mxq(w1.T, 0, "e4m3")) + f64(b1), 0.0)
    logits = (mxq(h, 1, "e4m3") @ mxq(f64(W2).T, 0, "e4m3")) + f64(b2)
    return logits.reshape(B, H, W, C).transpose(0, 3, 1, 2)

@@ -1,0 +1,246 @@
+from contextlib import ExitStack
+
+import concourse.mybir as mybir
+from concourse.masks import make_identity
+
+BF16 = mybir.dt.bfloat16
+F32 = mybir.dt.float32
+I32 = mybir.dt.int32
+U32 = mybir.dt.uint32
+U8 = mybir.dt.uint8
+FP8X4 = mybir.dt.float8_e4m3fn_x4
+ACT = mybir.ActivationFunctionType
+
+P = 128
+PACK = 4
+BATCH, CHANNELS, SIDE, HIDDEN = 2, 2048, 16, 512
+WINDOW = 9
+IMAGE = SIDE * SIDE
+PIXELS = BATCH * IMAGE
+
+QUADS = 4
+HALVES = 2
+A_HALF = 64
+HALF_COLUMNS = A_HALF * 16 * WINDOW
+
+WORDS = 4
+WORD_POSITIONS = [[3 * di, 3 * di + 2] for di in range(3)] + [[1, 7]]
+PLANES = 2 * WORDS
+VECTOR_PLANES = 6
+
+D_TILES = HIDDEN // P
+K_GROUPS = CHANNELS // (2 * P)
+
+FLOPS = 2 * PIXELS * HIDDEN * (8 * CHANNELS) + 2 * PIXELS * HIDDEN * CHANNELS
+
+
+def turn_and_quantise(nc, ident, turn_pool, grouped_pool, planes, codes, scales):
+    grouped = grouped_pool.tile([P, 2, 2, P, PACK], BF16, align_bytes=64, tag="grouped")
+    for bank in range(2):
+        turned = turn_pool.tile([P, 4, P], F32, tag="turned")
+        for k in range(4):
+            nc.tensor.transpose(turned[:, k, :], planes[4 * bank + k], ident)
+        nc.scalar.copy(
+            out=grouped[:, bank].bitcast(F32),
+            in_=turned[:].rearrange("p (s u) d -> p s d u", u=2),
+        )
+    nc.vector.quantize_mx(
+        out=codes.bitcast(FP8X4),
+        scales=scales,
+        in_=grouped[:].rearrange("p a s d t -> p (a s d t)"),
+    )
+
+
+def tile_localpredictor_pa_k_kernel(tc, z, W1, b1, W2, b2, out):
+    nc = tc.nc
+    z_view = z.rearrange("b (a q r j) h w -> q r a b (j h w)", a=HALVES * A_HALF, q=QUADS, r=2, j=2)
+    w1_view = W1.rearrange("(u p e) k -> u e p k", u=2, p=P, e=2)
+    w2_view = W2.rearrange("(g p e) d -> p g (e d)", g=K_GROUPS, p=P, e=2)
+    out_view = out.rearrange("b (g p e) h w -> g p b (e h w)", g=K_GROUPS, p=P, e=2)
+
+    with ExitStack() as ctx:
+        keep = ctx.enter_context(tc.tile_pool(name="keep", bufs=1))
+        z_pool = ctx.enter_context(tc.tile_pool(name="z", bufs=4))
+        raw_pool = ctx.enter_context(tc.tile_pool(name="raw", bufs=2))
+        sorted_pool = ctx.enter_context(tc.tile_pool(name="sorted", bufs=2))
+        grouped_pool = ctx.enter_context(tc.tile_pool(name="grouped", bufs=3))
+        w1q_pool = ctx.enter_context(tc.tile_pool(name="w1q", bufs=3))
+        res_pool = ctx.enter_context(tc.tile_pool(name="res", bufs=3))
+        turn_pool = ctx.enter_context(tc.psum_pool(name="turn", bufs=4))
+        sum_pool = ctx.enter_context(tc.psum_pool(name="sums", bufs=D_TILES))
+
+        ident = keep.tile([P, P], F32)
+        make_identity(nc, ident[:])
+
+        side_tiles = [
+            keep.tile([P, BATCH, SIDE + 2, SIDE, PACK], BF16, align_bytes=64, name="side%d" % i) for i in range(2)
+        ]
+        updown_tiles = [
+            keep.tile([P, BATCH, SIDE, SIDE, PACK], BF16, align_bytes=64, name="updown%d" % i) for i in range(2)
+        ]
+        for window_tile in side_tiles + updown_tiles:
+            nc.vector.memset(window_tile[:].bitcast(I32), 0)
+        win_codes = keep.tile([P, HALVES * QUADS, WORDS, PIXELS], U32, align_bytes=64)
+        win_scales = keep.tile([P, HALVES * QUADS, WORDS, PIXELS], U8, align_bytes=64)
+
+        def load_maps(half, q):
+            maps = z_pool.tile([P, BATCH, 2, SIDE, SIDE], BF16, tag="maps")
+            for r in range(2):
+                nc.sync.dma_start(
+                    out=maps[r:P:2, :, :, :, :].rearrange("p b j h w -> p b (j h w)"),
+                    in_=z_view[q, r, A_HALF * half : A_HALF * (half + 1)],
+                )
+            return maps
+
+        def build_windows(tau, maps):
+            side = side_tiles[tau % 2]
+            updown = updown_tiles[tau % 2]
+            for b in range(BATCH):
+                by_pixel = maps[:, b].rearrange("p j h w -> p h w j")
+                nc.vector.tensor_copy(out=side[:, b, 1 : SIDE + 1, 1:SIDE, 0:2], in_=by_pixel[:, :, 0 : SIDE - 1, :])
+                nc.vector.tensor_copy(out=side[:, b, 1 : SIDE + 1, 0 : SIDE - 1, 2:4], in_=by_pixel[:, :, 1:SIDE, :])
+                nc.scalar.copy(out=updown[:, b, 1:SIDE, :, 0:2], in_=by_pixel[:, 0 : SIDE - 1, :, :])
+                nc.scalar.copy(out=updown[:, b, 0 : SIDE - 1, :, 2:4], in_=by_pixel[:, 1:SIDE, :, :])
+
+        def quantise_windows(tau):
+            side = side_tiles[tau % 2]
+            updown = updown_tiles[tau % 2]
+            for b in range(BATCH):
+                pixels = slice(IMAGE * b, IMAGE * (b + 1))
+                words = [side[:, b, di : di + SIDE] for di in range(3)] + [updown[:, b]]
+                for s in range(WORDS):
+                    nc.vector.quantize_mx(
+                        out=win_codes[:, tau, s, pixels].bitcast(FP8X4),
+                        scales=win_scales[:, tau, s, pixels],
+                        in_=words[s].rearrange("p h w t -> p (h w t)"),
+                    )
+
+
+        def load_chunk(chunk):
+            half, d_tile = divmod(chunk, D_TILES)
+            u, e = divmod(d_tile, 2)
+            raw = raw_pool.tile([P, HALF_COLUMNS], BF16, tag="raw")
+            nc.sync.dma_start(out=raw[:], in_=w1_view[u, e, :, HALF_COLUMNS * half : HALF_COLUMNS * (half + 1)])
+            return raw
+
+        def sort_chunk(raw):
+            by_position = raw[:].rearrange("d (a q c k) -> d k q a c", a=A_HALF, q=QUADS, c=4, k=WINDOW)
+            ordered = sorted_pool.tile([P, QUADS, PLANES, 2 * P], BF16, tag="ordered")
+            for n in range(PLANES):
+                plane = ordered[:, :, n, :].rearrange("d q (a c) -> d q a c", c=4)
+                column = by_position[:, WORD_POSITIONS[n // 2][n % 2]]
+                if n < VECTOR_PLANES:
+                    nc.vector.tensor_copy(out=plane, in_=column)
+                else:
+                    nc.scalar.copy(out=plane, in_=column)
+            return ordered
+
+        def multiply_chunk(chunk, ordered, acc):
+            half = chunk // D_TILES
+            for q in range(QUADS):
+                w1_codes = w1q_pool.tile([P, WORDS * P], U32, align_bytes=64, tag="w1_codes")
+                w1_scales = w1q_pool.tile([P, WORDS * P], U8, align_bytes=64, tag="w1_scales")
+                planes = [ordered[:, q, n, :].bitcast(F32) for n in range(PLANES)]
+                turn_and_quantise(nc, ident[:], turn_pool, grouped_pool, planes, w1_codes[:], w1_scales[:])
+                tau = QUADS * half + q
+                for s in range(WORDS):
+                    rows = slice(P * s, P * (s + 1))
+                    nc.tensor.matmul_mx(
+                        out=acc[:],
+                        lhsT=w1_codes[:, rows].bitcast(FP8X4),
+                        lhsT_scale=w1_scales[:, rows],
+                        rhs=win_codes[:, tau, s, :].bitcast(FP8X4),
+                        rhs_scale=win_scales[:, tau, s, :],
+                        start=(half == 0 and q == 0 and s == 0),
+                        stop=(half == HALVES - 1 and q == QUADS - 1 and s == WORDS - 1),
+                    )
+
+        bias_rows = keep.tile([P, 2 * P], BF16)
+        nc.vector.memset(bias_rows[:].bitcast(I32), 0)
+        nc.sync.dma_start(out=bias_rows[0:2, :], in_=b1.rearrange("(u x) -> u x", u=2))
+        nc.sync.dma_start(out=bias_rows[2 : 2 + K_GROUPS, :], in_=b2.rearrange("(g x) -> g x", g=K_GROUPS))
+
+        maps = [load_maps(0, q) for q in range(QUADS)]
+        for q in range(QUADS + 1):
+            if q < QUADS:
+                build_windows(q, maps[q])
+            if q > 0:
+                quantise_windows(q - 1)
+
+        w2_raw = raw_pool.tile([P, K_GROUPS, 2, HIDDEN], BF16, tag="raw")
+        nc.sync.dma_start(out=w2_raw[:].rearrange("p g e d -> p g (e d)"), in_=w2_view)
+        raw = load_chunk(0)
+
+        bias_turned = turn_pool.tile([P, 4, P], F32, tag="turned")
+        nc.tensor.transpose(bias_turned[:, 0, :], bias_rows[:].bitcast(F32), ident[:])
+        bias = keep.tile([P, 2 * (2 + K_GROUPS)], F32)
+        nc.vector.tensor_copy(out=bias[:], in_=bias_turned[:, 0, 0 : 2 + K_GROUPS].bitcast(BF16))
+
+        w2_codes = keep.tile([P, 2 * K_GROUPS * P], U32, align_bytes=64)
+        w2_scales = keep.tile([P, 2 * K_GROUPS * P], U8, align_bytes=64)
+        for call in range(K_GROUPS // 2):
+            planes = [
+                w2_raw[:, 2 * call + g, e, 2 * P * u : 2 * P * (u + 1)].bitcast(F32)
+                for g in range(2)
+                for e in range(2)
+                for u in range(2)
+            ]
+            columns = slice(WORDS * P * call, WORDS * P * (call + 1))
+            turn_and_quantise(nc, ident[:], turn_pool, grouped_pool, planes, w2_codes[:, columns], w2_scales[:, columns])
+
+        hidden = keep.tile([P, D_TILES, PIXELS], BF16)
+        sums = [sum_pool.tile([P, PIXELS], F32, tag="sums", name="hidden_sums%d" % i) for i in range(D_TILES)]
+        maps = [load_maps(1, q) for q in range(QUADS)]
+        ordered = sort_chunk(raw)
+        next_ordered = ordered
+        for chunk in range(HALVES * D_TILES):
+            half, d_tile = divmod(chunk, D_TILES)
+            if half == 0:
+                build_windows(QUADS + d_tile, maps[d_tile])
+            if chunk + 1 < HALVES * D_TILES:
+                next_ordered = sort_chunk(load_chunk(chunk + 1))
+            if half == 0:
+                quantise_windows(QUADS + d_tile)
+            multiply_chunk(chunk, ordered, sums[d_tile])
+            if half == HALVES - 1:
+                nc.scalar.activation(
+                    out=hidden[:, d_tile, :],
+                    in_=sums[d_tile][:],
+                    func=ACT.Relu,
+                    bias=bias[:, d_tile : d_tile + 1],
+                    scale=1.0,
+                )
+            ordered = next_ordered
+
+        hidden_grouped = grouped_pool.tile([P, PIXELS, PACK], BF16, align_bytes=64, tag="grouped")
+        nc.vector.tensor_copy(out=hidden_grouped[:], in_=hidden[:].rearrange("p t x -> p x t"))
+        hidden_codes = keep.tile([P, PIXELS], U32, align_bytes=64)
+        hidden_scales = keep.tile([P, PIXELS], U8, align_bytes=64)
+        nc.vector.quantize_mx(
+            out=hidden_codes[:].bitcast(FP8X4),
+            scales=hidden_scales[:],
+            in_=hidden_grouped[:].rearrange("p x t -> p (x t)"),
+        )
+
+        for g in range(K_GROUPS):
+            res = res_pool.tile([P, BATCH, 2, IMAGE], F32, tag="res")
+            for e in range(2):
+                k_tile = 2 * g + e
+                rows = slice(P * k_tile, P * (k_tile + 1))
+                logits = sum_pool.tile([P, PIXELS], F32, tag="sums")
+                nc.tensor.matmul_mx(
+                    out=logits[:],
+                    lhsT=w2_codes[:, rows].bitcast(FP8X4),
+                    lhsT_scale=w2_scales[:, rows],
+                    rhs=hidden_codes[:].bitcast(FP8X4),
+                    rhs_scale=hidden_scales[:],
+                    start=True,
+                    stop=True,
+                )
+                by_image = logits[:].rearrange("p (b x) -> p b x", b=BATCH)
+                b2_column = bias[:, 4 + k_tile : 5 + k_tile]
+                if e == 0:
+                    nc.scalar.activation(out=res[:, :, e, :], in_=by_image, func=ACT.Identity, bias=b2_column, scale=1.0)
+                else:
+                    nc.vector.tensor_scalar_add(out=res[:, :, e, :], in0=by_image, scalar1=b2_column)
+            nc.sync.dma_start(out=out_view[g], in_=res[:].rearrange("p b e x -> p b (e x)"))

@@ -25,8 +25,8 @@ HALF_COLUMNS = A_HALF * 16 * WINDOW
 
 WORDS = 4
 WORD_POSITIONS = [[3 * di, 3 * di + 2] for di in range(3)] + [[1, 7]]
-PLANES = 2 * WORDS
-VECTOR_PLANES = 6
+NEIGHBOURS = 2 * WORDS
+STEPS_AHEAD = 4
 
 D_TILES = HIDDEN // P
 K_GROUPS = CHANNELS // (2 * P)
@@ -62,7 +62,7 @@ def tile_localpredictor_pa_k_kernel(tc, z, W1, b1, W2, b2, out):
         keep = ctx.enter_context(tc.tile_pool(name="keep", bufs=1))
         z_pool = ctx.enter_context(tc.tile_pool(name="z", bufs=4))
         raw_pool = ctx.enter_context(tc.tile_pool(name="raw", bufs=2))
-        sorted_pool = ctx.enter_context(tc.tile_pool(name="sorted", bufs=2))
+        sorted_pool = ctx.enter_context(tc.tile_pool(name="sorted", bufs=STEPS_AHEAD + 2))
         grouped_pool = ctx.enter_context(tc.tile_pool(name="grouped", bufs=3))
         w1q_pool = ctx.enter_context(tc.tile_pool(name="w1q", bufs=3))
         res_pool = ctx.enter_context(tc.tile_pool(name="res", bufs=3))
@@ -123,37 +123,37 @@ def tile_localpredictor_pa_k_kernel(tc, z, W1, b1, W2, b2, out):
             nc.sync.dma_start(out=raw[:], in_=w1_view[u, e, :, HALF_COLUMNS * half : HALF_COLUMNS * (half + 1)])
             return raw
 
-        def sort_chunk(raw):
-            by_position = raw[:].rearrange("d (a q c k) -> d k q a c", a=A_HALF, q=QUADS, c=4, k=WINDOW)
-            ordered = sorted_pool.tile([P, QUADS, PLANES, 2 * P], BF16, tag="ordered")
-            for n in range(PLANES):
-                plane = ordered[:, :, n, :].rearrange("d q (a c) -> d q a c", c=4)
-                column = by_position[:, WORD_POSITIONS[n // 2][n % 2]]
-                if n < VECTOR_PLANES:
-                    nc.vector.tensor_copy(out=plane, in_=column)
+        def sort_step(raw, q):
+            by_channel = raw[:].rearrange("d (a q c k) -> d q a c k", a=A_HALF, q=QUADS, c=4, k=WINDOW)
+            ordered = sorted_pool.tile([P, NEIGHBOURS, 2 * P], BF16, tag="ordered")
+            for side_of_centre in range(2):
+                first = 4 * side_of_centre
+                planes = ordered[:, first : first + 4, :].rearrange("d k (a c) -> d a c k", c=4)
+                columns = by_channel[:, q, :, :, first + side_of_centre : first + side_of_centre + 4]
+                if side_of_centre == 1 and q % 2 == 1:
+                    nc.scalar.copy(out=planes, in_=columns)
                 else:
-                    nc.scalar.copy(out=plane, in_=column)
+                    nc.vector.tensor_copy(out=planes, in_=columns)
             return ordered
 
-        def multiply_chunk(chunk, ordered, acc):
-            half = chunk // D_TILES
-            for q in range(QUADS):
-                w1_codes = w1q_pool.tile([P, WORDS * P], U32, align_bytes=64, tag="w1_codes")
-                w1_scales = w1q_pool.tile([P, WORDS * P], U8, align_bytes=64, tag="w1_scales")
-                planes = [ordered[:, q, n, :].bitcast(F32) for n in range(PLANES)]
-                turn_and_quantise(nc, ident[:], turn_pool, grouped_pool, planes, w1_codes[:], w1_scales[:])
-                tau = QUADS * half + q
-                for s in range(WORDS):
-                    rows = slice(P * s, P * (s + 1))
-                    nc.tensor.matmul_mx(
-                        out=acc[:],
-                        lhsT=w1_codes[:, rows].bitcast(FP8X4),
-                        lhsT_scale=w1_scales[:, rows],
-                        rhs=win_codes[:, tau, s, :].bitcast(FP8X4),
-                        rhs_scale=win_scales[:, tau, s, :],
-                        start=(half == 0 and q == 0 and s == 0),
-                        stop=(half == HALVES - 1 and q == QUADS - 1 and s == WORDS - 1),
-                    )
+        def multiply_step(half, q, ordered, acc):
+            w1_codes = w1q_pool.tile([P, WORDS * P], U32, align_bytes=64, tag="w1_codes")
+            w1_scales = w1q_pool.tile([P, WORDS * P], U8, align_bytes=64, tag="w1_scales")
+            neighbour_of = [position - (position > WINDOW // 2) for pair in WORD_POSITIONS for position in pair]
+            planes = [ordered[:, n, :].bitcast(F32) for n in neighbour_of]
+            turn_and_quantise(nc, ident[:], turn_pool, grouped_pool, planes, w1_codes[:], w1_scales[:])
+            tau = QUADS * half + q
+            for s in range(WORDS):
+                rows = slice(P * s, P * (s + 1))
+                nc.tensor.matmul_mx(
+                    out=acc[:],
+                    lhsT=w1_codes[:, rows].bitcast(FP8X4),
+                    lhsT_scale=w1_scales[:, rows],
+                    rhs=win_codes[:, tau, s, :].bitcast(FP8X4),
+                    rhs_scale=win_scales[:, tau, s, :],
+                    start=(half == 0 and q == 0 and s == 0),
+                    stop=(half == HALVES - 1 and q == QUADS - 1 and s == WORDS - 1),
+                )
 
         bias_rows = keep.tile([P, 2 * P], BF16)
         nc.vector.memset(bias_rows[:].bitcast(I32), 0)
@@ -191,26 +191,32 @@ def tile_localpredictor_pa_k_kernel(tc, z, W1, b1, W2, b2, out):
         hidden = keep.tile([P, D_TILES, PIXELS], BF16)
         sums = [sum_pool.tile([P, PIXELS], F32, tag="sums", name="hidden_sums%d" % i) for i in range(D_TILES)]
         maps = [load_maps(1, q) for q in range(QUADS)]
-        ordered = sort_chunk(raw)
-        next_ordered = ordered
-        for chunk in range(HALVES * D_TILES):
-            half, d_tile = divmod(chunk, D_TILES)
-            if half == 0:
-                build_windows(QUADS + d_tile, maps[d_tile])
-            if chunk + 1 < HALVES * D_TILES:
-                next_ordered = sort_chunk(load_chunk(chunk + 1))
-            if half == 0:
-                quantise_windows(QUADS + d_tile)
-            multiply_chunk(chunk, ordered, sums[d_tile])
-            if half == HALVES - 1:
-                nc.scalar.activation(
-                    out=hidden[:, d_tile, :],
-                    in_=sums[d_tile][:],
-                    func=ACT.Relu,
-                    bias=bias[:, d_tile : d_tile + 1],
-                    scale=1.0,
-                )
-            ordered = next_ordered
+        chunks = HALVES * D_TILES
+        raws = [raw]
+        ordered_tiles = []
+        for step in range(-STEPS_AHEAD, chunks * QUADS):
+            sorted_step = step + STEPS_AHEAD
+            if sorted_step < chunks * QUADS:
+                chunk, q = divmod(sorted_step, QUADS)
+                if q == 0 and chunk + 1 < chunks:
+                    raws.append(load_chunk(chunk + 1))
+                ordered_tiles.append(sort_step(raws[chunk], q))
+            if step >= 0:
+                chunk, q = divmod(step, QUADS)
+                half, d_tile = divmod(chunk, D_TILES)
+                if half == 0 and q == 0:
+                    build_windows(QUADS + d_tile, maps[d_tile])
+                if half == 0 and q == 2:
+                    quantise_windows(QUADS + d_tile)
+                multiply_step(half, q, ordered_tiles[step], sums[d_tile])
+                if half == HALVES - 1 and q == QUADS - 1:
+                    nc.scalar.activation(
+                        out=hidden[:, d_tile, :],
+                        in_=sums[d_tile][:],
+                        func=ACT.Relu,
+                        bias=bias[:, d_tile : d_tile + 1],
+                        scale=1.0,
+                    )
 
         hidden_grouped = grouped_pool.tile([P, PIXELS, PACK], BF16, align_bytes=64, tag="grouped")
         nc.vector.tensor_copy(out=hidden_grouped[:], in_=hidden[:].rearrange("p t x -> p x t"))

@@ -26,29 +26,19 @@ HALF_COLUMNS = A_HALF * 16 * WINDOW
 WORDS = 4
 WORD_POSITIONS = [[3 * di, 3 * di + 2] for di in range(3)] + [[1, 7]]
 NEIGHBOURS = 2 * WORDS
-STEPS_AHEAD = 4
+
+CHUNKS = HALVES * (HIDDEN // P)
+STEPS = CHUNKS * QUADS
+SORT_AHEAD = 4
+W2_CALLS = 4
+FIRST_W2_ITEM = -8
+TILES = HALVES * QUADS
+PIECES = 4
 
 D_TILES = HIDDEN // P
 K_GROUPS = CHANNELS // (2 * P)
 
 FLOPS = 2 * PIXELS * HIDDEN * (8 * CHANNELS) + 2 * PIXELS * HIDDEN * CHANNELS
-
-
-def turn_and_quantise(nc, ident, turn_pool, grouped_pool, planes, codes, scales):
-    grouped = grouped_pool.tile([P, 2, 2, P, PACK], BF16, align_bytes=64, tag="grouped")
-    for bank in range(2):
-        turned = turn_pool.tile([P, 4, P], F32, tag="turned")
-        for k in range(4):
-            nc.tensor.transpose(turned[:, k, :], planes[4 * bank + k], ident)
-        nc.scalar.copy(
-            out=grouped[:, bank].bitcast(F32),
-            in_=turned[:].rearrange("p (s u) d -> p s d u", u=2),
-        )
-    nc.vector.quantize_mx(
-        out=codes.bitcast(FP8X4),
-        scales=scales,
-        in_=grouped[:].rearrange("p a s d t -> p (a s d t)"),
-    )
 
 
 def tile_localpredictor_pa_k_kernel(tc, z, W1, b1, W2, b2, out):
@@ -60,17 +50,46 @@ def tile_localpredictor_pa_k_kernel(tc, z, W1, b1, W2, b2, out):
 
     with ExitStack() as ctx:
         keep = ctx.enter_context(tc.tile_pool(name="keep", bufs=1))
-        z_pool = ctx.enter_context(tc.tile_pool(name="z", bufs=4))
+        z_pool = ctx.enter_context(tc.tile_pool(name="z", bufs=TILES))
         raw_pool = ctx.enter_context(tc.tile_pool(name="raw", bufs=2))
-        sorted_pool = ctx.enter_context(tc.tile_pool(name="sorted", bufs=STEPS_AHEAD + 2))
+        sorted_pool = ctx.enter_context(tc.tile_pool(name="sorted", bufs=SORT_AHEAD + 2))
         grouped_pool = ctx.enter_context(tc.tile_pool(name="grouped", bufs=3))
         w1q_pool = ctx.enter_context(tc.tile_pool(name="w1q", bufs=3))
         res_pool = ctx.enter_context(tc.tile_pool(name="res", bufs=3))
         turn_pool = ctx.enter_context(tc.psum_pool(name="turn", bufs=4))
         sum_pool = ctx.enter_context(tc.psum_pool(name="sums", bufs=D_TILES))
+        ctx.enter_context(tc.manual_schedule())
 
         ident = keep.tile([P, P], F32)
         make_identity(nc, ident[:])
+
+        bias_rows = keep.tile([P, 2 * P], BF16)
+        nc.vector.memset(bias_rows[:].bitcast(I32), 0)
+        nc.sync.dma_start(out=bias_rows[0:2, :], in_=b1.rearrange("(u x) -> u x", u=2))
+        nc.sync.dma_start(out=bias_rows[2 : 2 + K_GROUPS, :], in_=b2.rearrange("(g x) -> g x", g=K_GROUPS))
+
+        def load_maps(tile_index):
+            half, q = divmod(tile_index, QUADS)
+            maps = z_pool.tile([P, BATCH, 2, SIDE, SIDE], BF16, tag="maps")
+            for r in range(2):
+                nc.sync.dma_start(
+                    out=maps[r:P:2, :, :, :, :].rearrange("p b j h w -> p b (j h w)"),
+                    in_=z_view[q, r, A_HALF * half : A_HALF * (half + 1)],
+                )
+            return maps
+
+        def load_chunk(chunk):
+            half, d_tile = divmod(chunk, D_TILES)
+            u, e = divmod(d_tile, 2)
+            raw = raw_pool.tile([P, HALF_COLUMNS], BF16, tag="raw")
+            nc.sync.dma_start(out=raw[:], in_=w1_view[u, e, :, HALF_COLUMNS * half : HALF_COLUMNS * (half + 1)])
+            return raw
+
+        maps = [load_maps(tile_index) for tile_index in range(QUADS)]
+        w2_raw = raw_pool.tile([P, K_GROUPS, 2, HIDDEN], BF16, tag="raw")
+        nc.sync.dma_start(out=w2_raw[:].rearrange("p g e d -> p g (e d)"), in_=w2_view)
+        raws = [load_chunk(0)]
+        maps = maps + [load_maps(tile_index) for tile_index in range(QUADS, TILES)]
 
         side_tiles = [
             keep.tile([P, BATCH, SIDE + 2, SIDE, PACK], BF16, align_bytes=64, name="side%d" % i) for i in range(2)
@@ -80,51 +99,38 @@ def tile_localpredictor_pa_k_kernel(tc, z, W1, b1, W2, b2, out):
         ]
         for window_tile in side_tiles + updown_tiles:
             nc.vector.memset(window_tile[:].bitcast(I32), 0)
-        win_codes = keep.tile([P, HALVES * QUADS, WORDS, PIXELS], U32, align_bytes=64)
-        win_scales = keep.tile([P, HALVES * QUADS, WORDS, PIXELS], U8, align_bytes=64)
+        win_codes = keep.tile([P, TILES, WORDS, PIXELS], U32, align_bytes=64)
+        win_scales = keep.tile([P, TILES, WORDS, PIXELS], U8, align_bytes=64)
 
-        def load_maps(half, q):
-            maps = z_pool.tile([P, BATCH, 2, SIDE, SIDE], BF16, tag="maps")
-            for r in range(2):
-                nc.sync.dma_start(
-                    out=maps[r:P:2, :, :, :, :].rearrange("p b j h w -> p b (j h w)"),
-                    in_=z_view[q, r, A_HALF * half : A_HALF * (half + 1)],
+        def build_windows(tile_index, piece):
+            b, u = divmod(piece, 2)
+            side = side_tiles[tile_index % 2]
+            updown = updown_tiles[tile_index % 2]
+            by_pixel = maps[tile_index][:, b].rearrange("p j h w -> p h w j")
+            values = slice(2 * u, 2 * u + 2)
+            kept = slice(u, SIDE - 1 + u)
+            served = slice(1 - u, SIDE - u)
+            nc.vector.tensor_copy(out=side[:, b, 1 : SIDE + 1, served, values], in_=by_pixel[:, :, kept, :])
+            nc.scalar.copy(out=updown[:, b, served, :, values], in_=by_pixel[:, kept, :, :])
+
+        def quantise_windows(tile_index, piece):
+            b, pair = divmod(piece, 2)
+            side = side_tiles[tile_index % 2]
+            updown = updown_tiles[tile_index % 2]
+            pixels = slice(IMAGE * b, IMAGE * (b + 1))
+            words = [side[:, b, di : di + SIDE] for di in range(3)] + [updown[:, b]]
+            for s in range(2 * pair, 2 * pair + 2):
+                nc.vector.quantize_mx(
+                    out=win_codes[:, tile_index, s, pixels].bitcast(FP8X4),
+                    scales=win_scales[:, tile_index, s, pixels],
+                    in_=words[s].rearrange("p h w t -> p (h w t)"),
                 )
-            return maps
 
-        def build_windows(tau, maps):
-            side = side_tiles[tau % 2]
-            updown = updown_tiles[tau % 2]
-            for b in range(BATCH):
-                by_pixel = maps[:, b].rearrange("p j h w -> p h w j")
-                nc.vector.tensor_copy(out=side[:, b, 1 : SIDE + 1, 1:SIDE, 0:2], in_=by_pixel[:, :, 0 : SIDE - 1, :])
-                nc.vector.tensor_copy(out=side[:, b, 1 : SIDE + 1, 0 : SIDE - 1, 2:4], in_=by_pixel[:, :, 1:SIDE, :])
-                nc.scalar.copy(out=updown[:, b, 1:SIDE, :, 0:2], in_=by_pixel[:, 0 : SIDE - 1, :, :])
-                nc.scalar.copy(out=updown[:, b, 0 : SIDE - 1, :, 2:4], in_=by_pixel[:, 1:SIDE, :, :])
+        ordered_tiles = {}
 
-        def quantise_windows(tau):
-            side = side_tiles[tau % 2]
-            updown = updown_tiles[tau % 2]
-            for b in range(BATCH):
-                pixels = slice(IMAGE * b, IMAGE * (b + 1))
-                words = [side[:, b, di : di + SIDE] for di in range(3)] + [updown[:, b]]
-                for s in range(WORDS):
-                    nc.vector.quantize_mx(
-                        out=win_codes[:, tau, s, pixels].bitcast(FP8X4),
-                        scales=win_scales[:, tau, s, pixels],
-                        in_=words[s].rearrange("p h w t -> p (h w t)"),
-                    )
-
-
-        def load_chunk(chunk):
-            half, d_tile = divmod(chunk, D_TILES)
-            u, e = divmod(d_tile, 2)
-            raw = raw_pool.tile([P, HALF_COLUMNS], BF16, tag="raw")
-            nc.sync.dma_start(out=raw[:], in_=w1_view[u, e, :, HALF_COLUMNS * half : HALF_COLUMNS * (half + 1)])
-            return raw
-
-        def sort_step(raw, q):
-            by_channel = raw[:].rearrange("d (a q c k) -> d q a c k", a=A_HALF, q=QUADS, c=4, k=WINDOW)
+        def sort_step(step):
+            chunk, q = divmod(step, QUADS)
+            by_channel = raws[chunk][:].rearrange("d (a q c k) -> d q a c k", a=A_HALF, q=QUADS, c=4, k=WINDOW)
             ordered = sorted_pool.tile([P, NEIGHBOURS, 2 * P], BF16, tag="ordered")
             for side_of_centre in range(2):
                 first = 4 * side_of_centre
@@ -134,89 +140,115 @@ def tile_localpredictor_pa_k_kernel(tc, z, W1, b1, W2, b2, out):
                     nc.scalar.copy(out=planes, in_=columns)
                 else:
                     nc.vector.tensor_copy(out=planes, in_=columns)
-            return ordered
+            ordered_tiles[step] = ordered
 
-        def multiply_step(half, q, ordered, acc):
-            w1_codes = w1q_pool.tile([P, WORDS * P], U32, align_bytes=64, tag="w1_codes")
-            w1_scales = w1q_pool.tile([P, WORDS * P], U8, align_bytes=64, tag="w1_scales")
-            neighbour_of = [position - (position > WINDOW // 2) for pair in WORD_POSITIONS for position in pair]
-            planes = [ordered[:, n, :].bitcast(F32) for n in neighbour_of]
-            turn_and_quantise(nc, ident[:], turn_pool, grouped_pool, planes, w1_codes[:], w1_scales[:])
-            tau = QUADS * half + q
+        w2_codes = keep.tile([P, 2 * K_GROUPS * P], U32, align_bytes=64)
+        w2_scales = keep.tile([P, 2 * K_GROUPS * P], U8, align_bytes=64)
+        neighbour_of = [position - (position > WINDOW // 2) for pair in WORD_POSITIONS for position in pair]
+
+        def is_item(item):
+            return FIRST_W2_ITEM <= item < FIRST_W2_ITEM + W2_CALLS or 0 <= item < STEPS
+
+        def planes_of(item):
+            if item >= 0:
+                return [ordered_tiles[item][:, n, :].bitcast(F32) for n in neighbour_of]
+            call = item - FIRST_W2_ITEM
+            return [
+                w2_raw[:, 2 * call + g, e, 2 * P * u : 2 * P * (u + 1)].bitcast(F32)
+                for g in range(2)
+                for e in range(2)
+                for u in range(2)
+            ]
+
+        turned_tiles = {}
+        grouped_tiles = {}
+        codes_of = {}
+
+        def turn(item):
+            planes = planes_of(item)
+            turned_tiles[item] = []
+            for bank in range(2):
+                turned = turn_pool.tile([P, 4, P], F32, tag="turned")
+                for k in range(4):
+                    nc.tensor.transpose(turned[:, k, :], planes[4 * bank + k], ident[:])
+                turned_tiles[item].append(turned)
+
+        def drain(item):
+            grouped = grouped_pool.tile([P, 2, 2, P, PACK], BF16, align_bytes=64, tag="grouped")
+            for bank in range(2):
+                nc.scalar.copy(
+                    out=grouped[:, bank].bitcast(F32),
+                    in_=turned_tiles[item][bank][:].rearrange("p (s u) d -> p s d u", u=2),
+                )
+            grouped_tiles[item] = grouped
+
+        def quantise(item):
+            if item >= 0:
+                codes = w1q_pool.tile([P, WORDS * P], U32, align_bytes=64, tag="w1_codes")
+                scales = w1q_pool.tile([P, WORDS * P], U8, align_bytes=64, tag="w1_scales")
+                codes_of[item] = (codes[:], scales[:])
+            else:
+                columns = slice(WORDS * P * (item - FIRST_W2_ITEM), WORDS * P * (item - FIRST_W2_ITEM + 1))
+                codes_of[item] = (w2_codes[:, columns], w2_scales[:, columns])
+            nc.vector.quantize_mx(
+                out=codes_of[item][0].bitcast(FP8X4),
+                scales=codes_of[item][1],
+                in_=grouped_tiles[item][:].rearrange("p a s d t -> p (a s d t)"),
+            )
+
+        sums = [sum_pool.tile([P, PIXELS], F32, tag="sums", name="hidden_sums%d" % i) for i in range(D_TILES)]
+        hidden = keep.tile([P, D_TILES, PIXELS], BF16)
+
+        def multiply(step):
+            chunk, q = divmod(step, QUADS)
+            half, d_tile = divmod(chunk, D_TILES)
+            codes, scales = codes_of[step]
             for s in range(WORDS):
                 rows = slice(P * s, P * (s + 1))
                 nc.tensor.matmul_mx(
-                    out=acc[:],
-                    lhsT=w1_codes[:, rows].bitcast(FP8X4),
-                    lhsT_scale=w1_scales[:, rows],
-                    rhs=win_codes[:, tau, s, :].bitcast(FP8X4),
-                    rhs_scale=win_scales[:, tau, s, :],
+                    out=sums[d_tile][:],
+                    lhsT=codes[:, rows].bitcast(FP8X4),
+                    lhsT_scale=scales[:, rows],
+                    rhs=win_codes[:, QUADS * half + q, s, :].bitcast(FP8X4),
+                    rhs_scale=win_scales[:, QUADS * half + q, s, :],
                     start=(half == 0 and q == 0 and s == 0),
                     stop=(half == HALVES - 1 and q == QUADS - 1 and s == WORDS - 1),
                 )
-
-        bias_rows = keep.tile([P, 2 * P], BF16)
-        nc.vector.memset(bias_rows[:].bitcast(I32), 0)
-        nc.sync.dma_start(out=bias_rows[0:2, :], in_=b1.rearrange("(u x) -> u x", u=2))
-        nc.sync.dma_start(out=bias_rows[2 : 2 + K_GROUPS, :], in_=b2.rearrange("(g x) -> g x", g=K_GROUPS))
-
-        maps = [load_maps(0, q) for q in range(QUADS)]
-        for q in range(QUADS + 1):
-            if q < QUADS:
-                build_windows(q, maps[q])
-            if q > 0:
-                quantise_windows(q - 1)
-
-        w2_raw = raw_pool.tile([P, K_GROUPS, 2, HIDDEN], BF16, tag="raw")
-        nc.sync.dma_start(out=w2_raw[:].rearrange("p g e d -> p g (e d)"), in_=w2_view)
-        raw = load_chunk(0)
 
         bias_turned = turn_pool.tile([P, 4, P], F32, tag="turned")
         nc.tensor.transpose(bias_turned[:, 0, :], bias_rows[:].bitcast(F32), ident[:])
         bias = keep.tile([P, 2 * (2 + K_GROUPS)], F32)
         nc.vector.tensor_copy(out=bias[:], in_=bias_turned[:, 0, 0 : 2 + K_GROUPS].bitcast(BF16))
 
-        w2_codes = keep.tile([P, 2 * K_GROUPS * P], U32, align_bytes=64)
-        w2_scales = keep.tile([P, 2 * K_GROUPS * P], U8, align_bytes=64)
-        for call in range(K_GROUPS // 2):
-            planes = [
-                w2_raw[:, 2 * call + g, e, 2 * P * u : 2 * P * (u + 1)].bitcast(F32)
-                for g in range(2)
-                for e in range(2)
-                for u in range(2)
-            ]
-            columns = slice(WORDS * P * call, WORDS * P * (call + 1))
-            turn_and_quantise(nc, ident[:], turn_pool, grouped_pool, planes, w2_codes[:, columns], w2_scales[:, columns])
-
-        hidden = keep.tile([P, D_TILES, PIXELS], BF16)
-        sums = [sum_pool.tile([P, PIXELS], F32, tag="sums", name="hidden_sums%d" % i) for i in range(D_TILES)]
-        maps = [load_maps(1, q) for q in range(QUADS)]
-        chunks = HALVES * D_TILES
-        raws = [raw]
-        ordered_tiles = []
-        for step in range(-STEPS_AHEAD, chunks * QUADS):
-            sorted_step = step + STEPS_AHEAD
-            if sorted_step < chunks * QUADS:
-                chunk, q = divmod(sorted_step, QUADS)
-                if q == 0 and chunk + 1 < chunks:
+        for t in range(-PIECES * QUADS, STEPS + 3):
+            if is_item(t + 1):
+                turn(t + 1)
+            if is_item(t):
+                drain(t)
+            if is_item(t - 1):
+                quantise(t - 1)
+            if 0 <= t - 2 < STEPS:
+                multiply(t - 2)
+            finished_chunk, last = divmod(t - 3, QUADS)
+            if last == QUADS - 1 and D_TILES <= finished_chunk < CHUNKS:
+                d_tile = finished_chunk - D_TILES
+                nc.scalar.activation(
+                    out=hidden[:, d_tile, :],
+                    in_=sums[d_tile][:],
+                    func=ACT.Relu,
+                    bias=bias[:, d_tile : d_tile + 1],
+                    scale=1.0,
+                )
+            if 0 <= t + SORT_AHEAD < STEPS:
+                chunk, q = divmod(t + SORT_AHEAD, QUADS)
+                if q == 0 and chunk + 1 < CHUNKS:
                     raws.append(load_chunk(chunk + 1))
-                ordered_tiles.append(sort_step(raws[chunk], q))
-            if step >= 0:
-                chunk, q = divmod(step, QUADS)
-                half, d_tile = divmod(chunk, D_TILES)
-                if half == 0 and q == 0:
-                    build_windows(QUADS + d_tile, maps[d_tile])
-                if half == 0 and q == 2:
-                    quantise_windows(QUADS + d_tile)
-                multiply_step(half, q, ordered_tiles[step], sums[d_tile])
-                if half == HALVES - 1 and q == QUADS - 1:
-                    nc.scalar.activation(
-                        out=hidden[:, d_tile, :],
-                        in_=sums[d_tile][:],
-                        func=ACT.Relu,
-                        bias=bias[:, d_tile : d_tile + 1],
-                        scale=1.0,
-                    )
+                sort_step(t + SORT_AHEAD)
+            slot, piece = divmod(t, PIECES)
+            if 0 <= slot + QUADS < TILES:
+                build_windows(slot + QUADS, piece)
+            if 0 <= slot + QUADS - 1 < TILES:
+                quantise_windows(slot + QUADS - 1, piece)
 
         hidden_grouped = grouped_pool.tile([P, PIXELS, PACK], BF16, align_bytes=64, tag="grouped")
         nc.vector.tensor_copy(out=hidden_grouped[:], in_=hidden[:].rearrange("p t x -> p x t"))

@@ -18,24 +18,28 @@ WINDOW = 9
 IMAGE = SIDE * SIDE
 PIXELS = BATCH * IMAGE
 
-QUADS = 4
-HALVES = 2
-A_HALF = 64
-HALF_COLUMNS = A_HALF * 16 * WINDOW
+GROUPS = 4
+GROUP_CHANNELS = CHANNELS // GROUPS
+A = GROUP_CHANNELS // 16
+GROUP_COLUMNS = GROUP_CHANNELS * WINDOW
+TILES = 2 * GROUPS
+
+HALF_SIDE = SIDE // 2
+PITCH = 32
+FIRST = 8
 
 WORDS = 4
-WORD_POSITIONS = [[3 * di, 3 * di + 2] for di in range(3)] + [[1, 7]]
-NEIGHBOURS = 2 * WORDS
-
-CHUNKS = HALVES * (HIDDEN // P)
-STEPS = CHUNKS * QUADS
-SORT_AHEAD = 4
-W2_CALLS = 4
-FIRST_W2_ITEM = -8
-TILES = HALVES * QUADS
-PIECES = 4
+NEIGHBOURS = 8
 
 D_TILES = HIDDEN // P
+CHUNKS = GROUPS * D_TILES
+STEPS = 2 * CHUNKS
+SORT_AHEAD = 3
+W2_CALLS = 4
+FIRST_W2_ITEM = -4
+PIECES = 4
+RAW_AHEAD = 3
+
 K_GROUPS = CHANNELS // (2 * P)
 
 FLOPS = 2 * PIXELS * HIDDEN * (8 * CHANNELS) + 2 * PIXELS * HIDDEN * CHANNELS
@@ -43,7 +47,7 @@ FLOPS = 2 * PIXELS * HIDDEN * (8 * CHANNELS) + 2 * PIXELS * HIDDEN * CHANNELS
 
 def tile_localpredictor_pa_k_kernel(tc, z, W1, b1, W2, b2, out):
     nc = tc.nc
-    z_view = z.rearrange("b (a q r j) h w -> q r a b (j h w)", a=HALVES * A_HALF, q=QUADS, r=2, j=2)
+    z_view = z.rearrange("b (g a s e r j) h w -> g s e r a b (j h w)", g=GROUPS, a=A, s=2, e=2, r=2, j=2)
     w1_view = W1.rearrange("(u p e) k -> u e p k", u=2, p=P, e=2)
     w2_view = W2.rearrange("(g p e) d -> p g (e d)", g=K_GROUPS, p=P, e=2)
     out_view = out.rearrange("b (g p e) h w -> g p b (e h w)", g=K_GROUPS, p=P, e=2)
@@ -51,7 +55,9 @@ def tile_localpredictor_pa_k_kernel(tc, z, W1, b1, W2, b2, out):
     with ExitStack() as ctx:
         keep = ctx.enter_context(tc.tile_pool(name="keep", bufs=1))
         z_pool = ctx.enter_context(tc.tile_pool(name="z", bufs=TILES))
-        raw_pool = ctx.enter_context(tc.tile_pool(name="raw", bufs=2))
+        raw_pool = ctx.enter_context(tc.tile_pool(name="raw", bufs=RAW_AHEAD + 1))
+        window_pool = ctx.enter_context(tc.tile_pool(name="window", bufs=2))
+        win_pool = ctx.enter_context(tc.tile_pool(name="win", bufs=4))
         sorted_pool = ctx.enter_context(tc.tile_pool(name="sorted", bufs=SORT_AHEAD + 2))
         grouped_pool = ctx.enter_context(tc.tile_pool(name="grouped", bufs=3))
         w1q_pool = ctx.enter_context(tc.tile_pool(name="w1q", bufs=3))
@@ -65,93 +71,128 @@ def tile_localpredictor_pa_k_kernel(tc, z, W1, b1, W2, b2, out):
 
         bias_rows = keep.tile([P, 2 * P], BF16)
         nc.vector.memset(bias_rows[:].bitcast(I32), 0)
-        nc.sync.dma_start(out=bias_rows[0:2, :], in_=b1.rearrange("(u x) -> u x", u=2))
-        nc.sync.dma_start(out=bias_rows[2 : 2 + K_GROUPS, :], in_=b2.rearrange("(g x) -> g x", g=K_GROUPS))
+
+        first_use = keep.tile([P, 1], F32)
+        nc.vector.memset(first_use[:], 0.0)
+        nc.scalar.activation(out=first_use[:], in_=first_use[:], func=ACT.Relu, scale=1.0)
 
         def load_maps(tile_index):
-            half, q = divmod(tile_index, QUADS)
+            group, half = divmod(tile_index, 2)
             maps = z_pool.tile([P, BATCH, 2, SIDE, SIDE], BF16, tag="maps")
-            for r in range(2):
-                nc.sync.dma_start(
-                    out=maps[r:P:2, :, :, :, :].rearrange("p b j h w -> p b (j h w)"),
-                    in_=z_view[q, r, A_HALF * half : A_HALF * (half + 1)],
-                )
+            for e in range(2):
+                for r in range(2):
+                    nc.sync.dma_start(
+                        out=maps[64 * e + r : 64 * (e + 1) : 2].rearrange("p b j h w -> p b (j h w)"),
+                        in_=z_view[group, half, e, r],
+                    )
             return maps
 
         def load_chunk(chunk):
-            half, d_tile = divmod(chunk, D_TILES)
+            group, d_tile = divmod(chunk, D_TILES)
             u, e = divmod(d_tile, 2)
-            raw = raw_pool.tile([P, HALF_COLUMNS], BF16, tag="raw")
-            nc.sync.dma_start(out=raw[:], in_=w1_view[u, e, :, HALF_COLUMNS * half : HALF_COLUMNS * (half + 1)])
+            raw = raw_pool.tile([P, GROUP_COLUMNS], BF16, tag="raw")
+            nc.sync.dma_start(out=raw[:], in_=w1_view[u, e, :, GROUP_COLUMNS * group : GROUP_COLUMNS * (group + 1)])
             return raw
 
-        maps = [load_maps(tile_index) for tile_index in range(QUADS)]
-        w2_raw = raw_pool.tile([P, K_GROUPS, 2, HIDDEN], BF16, tag="raw")
+        maps = [load_maps(0), load_maps(1)]
+        nc.sync.dma_start(out=bias_rows[0:2, :], in_=b1.rearrange("(u x) -> u x", u=2))
+        nc.sync.dma_start(out=bias_rows[2 : 2 + K_GROUPS, :], in_=b2.rearrange("(g x) -> g x", g=K_GROUPS))
+        w2_raw = keep.tile([P, K_GROUPS, 2, HIDDEN], BF16)
         nc.sync.dma_start(out=w2_raw[:].rearrange("p g e d -> p g (e d)"), in_=w2_view)
-        raws = [load_chunk(0)]
-        maps = maps + [load_maps(tile_index) for tile_index in range(QUADS, TILES)]
+        raws = [load_chunk(chunk) for chunk in range(RAW_AHEAD)]
+        maps = maps + [load_maps(2), load_maps(3)]
 
-        side_tiles = [
-            keep.tile([P, BATCH, SIDE + 2, SIDE, PACK], BF16, align_bytes=64, name="side%d" % i) for i in range(2)
-        ]
-        updown_tiles = [
-            keep.tile([P, BATCH, SIDE, SIDE, PACK], BF16, align_bytes=64, name="updown%d" % i) for i in range(2)
-        ]
-        for window_tile in side_tiles + updown_tiles:
-            nc.vector.memset(window_tile[:].bitcast(I32), 0)
-        win_codes = keep.tile([P, TILES, WORDS, PIXELS], U32, align_bytes=64)
-        win_scales = keep.tile([P, TILES, WORDS, PIXELS], U8, align_bytes=64)
+        padded_tiles = [keep.tile([P, 2, 2, SIDE + 2, BATCH, PITCH], BF16, name="padded%d" % i) for i in range(2)]
+        nc.vector.memset(padded_tiles[0][:].rearrange("p x j r b c -> p (x j r b c)").bitcast(I32), 0)
+        nc.gpsimd.memset(padded_tiles[1][:].rearrange("p x j r b c -> p (x j r b c)").bitcast(I32), 0)
 
-        def build_windows(tile_index, piece):
-            b, u = divmod(piece, 2)
-            side = side_tiles[tile_index % 2]
-            updown = updown_tiles[tile_index % 2]
-            by_pixel = maps[tile_index][:, b].rearrange("p j h w -> p h w j")
-            values = slice(2 * u, 2 * u + 2)
-            kept = slice(u, SIDE - 1 + u)
-            served = slice(1 - u, SIDE - u)
-            nc.vector.tensor_copy(out=side[:, b, 1 : SIDE + 1, served, values], in_=by_pixel[:, :, kept, :])
-            nc.scalar.copy(out=updown[:, b, served, :, values], in_=by_pixel[:, kept, :, :])
+        cross_of = {}
+        ends_of = {}
+        win_of = {}
 
-        def quantise_windows(tile_index, piece):
-            b, pair = divmod(piece, 2)
-            side = side_tiles[tile_index % 2]
-            updown = updown_tiles[tile_index % 2]
-            pixels = slice(IMAGE * b, IMAGE * (b + 1))
-            words = [side[:, b, di : di + SIDE] for di in range(3)] + [updown[:, b]]
-            for s in range(2 * pair, 2 * pair + 2):
-                nc.vector.quantize_mx(
-                    out=win_codes[:, tile_index, s, pixels].bitcast(FP8X4),
-                    scales=win_scales[:, tile_index, s, pixels],
-                    in_=words[s].rearrange("p h w t -> p (h w t)"),
+        def pad_maps(tile_index):
+            padded = padded_tiles[tile_index % 2]
+            by_row = maps[tile_index][:].rearrange("p b j h w -> p j h b w")
+            nc.scalar.copy(out=padded[:, 0, :, 1 : SIDE + 1, :, FIRST : FIRST + SIDE], in_=by_row)
+            nc.scalar.copy(out=padded[:, 1, :, 0:SIDE, :, FIRST + 2 : FIRST + 2 + SIDE], in_=by_row)
+
+        def build_cross(tile_index):
+            cross = window_pool.tile([P, SIDE + 1, BATCH, 2, HALF_SIDE, 2, 2], BF16, align_bytes=64, tag="cross")
+            pairs = padded_tiles[tile_index % 2][:, :, :, 0 : SIDE + 1, :, FIRST + 1 : FIRST + 1 + SIDE].rearrange(
+                "p x j r b (k y) -> p y r b k j x", y=2
+            )
+            for y in range(2):
+                nc.vector.tensor_copy(out=cross[:, :, :, y], in_=pairs[:, y])
+            cross_of[tile_index] = cross
+
+        def build_ends(tile_index, which, engine_copy):
+            if tile_index not in ends_of:
+                ends_of[tile_index] = window_pool.tile(
+                    [P, 2, SIDE, BATCH, 2, HALF_SIDE, 2, 2], BF16, align_bytes=64, tag="ends", name="ends"
                 )
+            ends = ends_of[tile_index]
+            for y in range(2):
+                place = FIRST - 1 + which + y
+                pairs = padded_tiles[tile_index % 2][
+                    :, 0, :, 2 * which : 2 * which + SIDE, :, place : place + SIDE
+                ].rearrange("p j r b (k x) -> p r b k j x", x=2)
+                engine_copy(out=ends[:, which, :, :, y], in_=pairs)
+
+        def quantise_windows(tile_index, words):
+            if tile_index not in win_of:
+                codes = win_pool.tile([P, WORDS, PIXELS], U32, align_bytes=64, tag="win_codes", name="win_codes")
+                scales = win_pool.tile([P, WORDS, PIXELS], U8, align_bytes=64, tag="win_scales", name="win_scales")
+                win_of[tile_index] = (codes, scales)
+            codes, scales = win_of[tile_index]
+            ends, cross = ends_of[tile_index], cross_of[tile_index]
+            sources = [ends[:, 0], cross[:, 0:SIDE], cross[:, 1 : SIDE + 1], ends[:, 1]]
+            for word in words:
+                nc.vector.quantize_mx(
+                    out=codes[:, word, :].bitcast(FP8X4),
+                    scales=scales[:, word, :],
+                    in_=sources[word].rearrange("p r b y k j x -> p (r b y k j x)"),
+                )
+
+        def window_piece(tile_index, piece):
+            if piece == 0:
+                build_cross(tile_index)
+                build_ends(tile_index, 0, nc.scalar.copy)
+            elif piece == 1:
+                build_ends(tile_index, 1, nc.vector.tensor_copy)
+            elif piece == 2:
+                quantise_windows(tile_index, [1, 2])
+            else:
+                quantise_windows(tile_index, [0, 3])
 
         ordered_tiles = {}
 
         def sort_step(step):
-            chunk, q = divmod(step, QUADS)
-            by_channel = raws[chunk][:].rearrange("d (a q c k) -> d q a c k", a=A_HALF, q=QUADS, c=4, k=WINDOW)
+            chunk, half = divmod(step, 2)
+            by_channel = raws[chunk][:].rearrange("d (a s e c k) -> d s e a c k", a=A, s=2, e=2, c=4, k=WINDOW)
             ordered = sorted_pool.tile([P, NEIGHBOURS, 2 * P], BF16, tag="ordered")
-            for side_of_centre in range(2):
-                first = 4 * side_of_centre
-                planes = ordered[:, first : first + 4, :].rearrange("d k (a c) -> d a c k", c=4)
-                columns = by_channel[:, q, :, :, first + side_of_centre : first + side_of_centre + 4]
-                if side_of_centre == 1 and q % 2 == 1:
-                    nc.scalar.copy(out=planes, in_=columns)
-                else:
-                    nc.vector.tensor_copy(out=planes, in_=columns)
+            for side in range(2):
+                runs = by_channel[:, half, :, :, :, 5 * side : 5 * side + 4]
+                planes = ordered[:, 4 * side : 4 * side + 4, :]
+                nc.vector.tensor_copy(
+                    out=planes.rearrange("d (j g) (e a r x) -> d e a r j g x", j=2, e=2, a=A, r=2),
+                    in_=runs.rearrange("d e a (r j) (g x) -> d e a r j g x", r=2, g=2),
+                )
             ordered_tiles[step] = ordered
 
         w2_codes = keep.tile([P, 2 * K_GROUPS * P], U32, align_bytes=64)
         w2_scales = keep.tile([P, 2 * K_GROUPS * P], U8, align_bytes=64)
-        neighbour_of = [position - (position > WINDOW // 2) for pair in WORD_POSITIONS for position in pair]
 
         def is_item(item):
             return FIRST_W2_ITEM <= item < FIRST_W2_ITEM + W2_CALLS or 0 <= item < STEPS
 
         def planes_of(item):
             if item >= 0:
-                return [ordered_tiles[item][:, n, :].bitcast(F32) for n in neighbour_of]
+                return [
+                    ordered_tiles[item][:, 4 * s + 2 * j + g, :].bitcast(F32)
+                    for s in range(2)
+                    for g in range(2)
+                    for j in range(2)
+                ]
             call = item - FIRST_W2_ITEM
             return [
                 w2_raw[:, 2 * call + g, e, 2 * P * u : 2 * P * (u + 1)].bitcast(F32)
@@ -200,27 +241,27 @@ def tile_localpredictor_pa_k_kernel(tc, z, W1, b1, W2, b2, out):
         hidden = keep.tile([P, D_TILES, PIXELS], BF16)
 
         def multiply(step):
-            chunk, q = divmod(step, QUADS)
-            half, d_tile = divmod(chunk, D_TILES)
+            chunk, half = divmod(step, 2)
+            group, d_tile = divmod(chunk, D_TILES)
             codes, scales = codes_of[step]
-            for s in range(WORDS):
-                rows = slice(P * s, P * (s + 1))
+            win_codes, win_scales = win_of[2 * group + half]
+            for word in range(WORDS):
+                rows = slice(P * word, P * (word + 1))
                 nc.tensor.matmul_mx(
                     out=sums[d_tile][:],
                     lhsT=codes[:, rows].bitcast(FP8X4),
                     lhsT_scale=scales[:, rows],
-                    rhs=win_codes[:, QUADS * half + q, s, :].bitcast(FP8X4),
-                    rhs_scale=win_scales[:, QUADS * half + q, s, :],
-                    start=(half == 0 and q == 0 and s == 0),
-                    stop=(half == HALVES - 1 and q == QUADS - 1 and s == WORDS - 1),
+                    rhs=win_codes[:, word, :].bitcast(FP8X4),
+                    rhs_scale=win_scales[:, word, :],
+                    start=(group == 0 and half == 0 and word == 0),
+                    stop=(group == GROUPS - 1 and half == 1 and word == WORDS - 1),
                 )
 
         bias_turned = turn_pool.tile([P, 4, P], F32, tag="turned")
         nc.tensor.transpose(bias_turned[:, 0, :], bias_rows[:].bitcast(F32), ident[:])
         bias = keep.tile([P, 2 * (2 + K_GROUPS)], F32)
-        nc.vector.tensor_copy(out=bias[:], in_=bias_turned[:, 0, 0 : 2 + K_GROUPS].bitcast(BF16))
 
-        for t in range(-PIECES * QUADS, STEPS + 3):
+        for t in range(-PIECES * 2 - 1, STEPS + 3):
             if is_item(t + 1):
                 turn(t + 1)
             if is_item(t):
@@ -229,26 +270,32 @@ def tile_localpredictor_pa_k_kernel(tc, z, W1, b1, W2, b2, out):
                 quantise(t - 1)
             if 0 <= t - 2 < STEPS:
                 multiply(t - 2)
-            finished_chunk, last = divmod(t - 3, QUADS)
-            if last == QUADS - 1 and D_TILES <= finished_chunk < CHUNKS:
-                d_tile = finished_chunk - D_TILES
-                nc.scalar.activation(
-                    out=hidden[:, d_tile, :],
-                    in_=sums[d_tile][:],
-                    func=ACT.Relu,
-                    bias=bias[:, d_tile : d_tile + 1],
-                    scale=1.0,
-                )
+            finished_chunk, last = divmod(t - 3, 2)
+            if last == 1 and CHUNKS - D_TILES <= finished_chunk < CHUNKS:
+                d_tile = finished_chunk % D_TILES
+                for b in range(BATCH):
+                    nc.scalar.activation(
+                        out=hidden[:, d_tile, IMAGE * b : IMAGE * (b + 1)].rearrange("p (r k y) -> p r k y", r=SIDE, y=2),
+                        in_=sums[d_tile][:].rearrange("p (r b y k) -> p b r k y", r=SIDE, b=BATCH, y=2)[:, b],
+                        func=ACT.Relu,
+                        bias=bias[:, d_tile : d_tile + 1],
+                        scale=1.0,
+                    )
             if 0 <= t + SORT_AHEAD < STEPS:
-                chunk, q = divmod(t + SORT_AHEAD, QUADS)
-                if q == 0 and chunk + 1 < CHUNKS:
-                    raws.append(load_chunk(chunk + 1))
+                chunk, half = divmod(t + SORT_AHEAD, 2)
+                if half == 0 and 1 <= chunk and chunk + RAW_AHEAD - 1 < CHUNKS:
+                    raws.append(load_chunk(chunk + RAW_AHEAD - 1))
+                    next_tile = 2 * (chunk // D_TILES) + 4
+                    if chunk % D_TILES == 1 and next_tile < TILES:
+                        maps = maps + [load_maps(next_tile), load_maps(next_tile + 1)]
                 sort_step(t + SORT_AHEAD)
+            if t == FIRST_W2_ITEM:
+                nc.vector.tensor_copy(out=bias[:], in_=bias_turned[:, 0, 0 : 2 + K_GROUPS].bitcast(BF16))
             slot, piece = divmod(t, PIECES)
-            if 0 <= slot + QUADS < TILES:
-                build_windows(slot + QUADS, piece)
-            if 0 <= slot + QUADS - 1 < TILES:
-                quantise_windows(slot + QUADS - 1, piece)
+            if 0 <= slot + 2 < TILES:
+                window_piece(slot + 2, piece)
+            if piece == PIECES - 1 and 0 <= slot + 3 < TILES:
+                pad_maps(slot + 3)
 
         hidden_grouped = grouped_pool.tile([P, PIXELS, PACK], BF16, align_bytes=64, tag="grouped")
         nc.vector.tensor_copy(out=hidden_grouped[:], in_=hidden[:].rearrange("p t x -> p x t"))

@@ -37,6 +37,7 @@ STEPS = 2 * CHUNKS
 SORT_AHEAD = 3
 W2_CALLS = 4
 FIRST_W2_ITEM = -4
+QUANTISE_W2 = 25
 PIECES = 4
 RAW_AHEAD = 3
 
@@ -60,6 +61,7 @@ def tile_localpredictor_pa_k_kernel(tc, z, W1, b1, W2, b2, out):
         win_pool = ctx.enter_context(tc.tile_pool(name="win", bufs=4))
         sorted_pool = ctx.enter_context(tc.tile_pool(name="sorted", bufs=SORT_AHEAD + 2))
         grouped_pool = ctx.enter_context(tc.tile_pool(name="grouped", bufs=3))
+        w2_grouped_pool = ctx.enter_context(tc.tile_pool(name="w2_grouped", bufs=W2_CALLS))
         w1q_pool = ctx.enter_context(tc.tile_pool(name="w1q", bufs=3))
         res_pool = ctx.enter_context(tc.tile_pool(name="res", bufs=3))
         turn_pool = ctx.enter_context(tc.psum_pool(name="turn", bufs=4))
@@ -173,7 +175,8 @@ def tile_localpredictor_pa_k_kernel(tc, z, W1, b1, W2, b2, out):
             for side in range(2):
                 runs = by_channel[:, half, :, :, :, 5 * side : 5 * side + 4]
                 planes = ordered[:, 4 * side : 4 * side + 4, :]
-                nc.vector.tensor_copy(
+                engine_copy = nc.scalar.copy if side == 1 and half == 1 else nc.vector.tensor_copy
+                engine_copy(
                     out=planes.rearrange("d (j g) (e a r x) -> d e a r j g x", j=2, e=2, a=A, r=2),
                     in_=runs.rearrange("d e a (r j) (g x) -> d e a r j g x", r=2, g=2),
                 )
@@ -215,7 +218,8 @@ def tile_localpredictor_pa_k_kernel(tc, z, W1, b1, W2, b2, out):
                 turned_tiles[item].append(turned)
 
         def drain(item):
-            grouped = grouped_pool.tile([P, 2, 2, P, PACK], BF16, align_bytes=64, tag="grouped")
+            pool = grouped_pool if item >= 0 else w2_grouped_pool
+            grouped = pool.tile([P, 2, 2, P, PACK], BF16, align_bytes=64, tag="grouped")
             for bank in range(2):
                 nc.scalar.copy(
                     out=grouped[:, bank].bitcast(F32),
@@ -261,12 +265,15 @@ def tile_localpredictor_pa_k_kernel(tc, z, W1, b1, W2, b2, out):
         nc.tensor.transpose(bias_turned[:, 0, :], bias_rows[:].bitcast(F32), ident[:])
         bias = keep.tile([P, 2 * (2 + K_GROUPS)], F32)
 
+        def first_window_tick(tile_index):
+            return PIECES * (tile_index - 2) + 1
+
         for t in range(-PIECES * 2 - 1, STEPS + 3):
             if is_item(t + 1):
                 turn(t + 1)
             if is_item(t):
                 drain(t)
-            if is_item(t - 1):
+            if 0 <= t - 1 < STEPS:
                 quantise(t - 1)
             if 0 <= t - 2 < STEPS:
                 multiply(t - 2)
@@ -291,11 +298,14 @@ def tile_localpredictor_pa_k_kernel(tc, z, W1, b1, W2, b2, out):
                 sort_step(t + SORT_AHEAD)
             if t == FIRST_W2_ITEM:
                 nc.vector.tensor_copy(out=bias[:], in_=bias_turned[:, 0, 0 : 2 + K_GROUPS].bitcast(BF16))
-            slot, piece = divmod(t, PIECES)
-            if 0 <= slot + 2 < TILES:
-                window_piece(slot + 2, piece)
-            if piece == PIECES - 1 and 0 <= slot + 3 < TILES:
-                pad_maps(slot + 3)
+            if 0 <= t - QUANTISE_W2 < W2_CALLS:
+                quantise(FIRST_W2_ITEM + t - QUANTISE_W2)
+            for tile_index in range(TILES):
+                piece = t - first_window_tick(tile_index)
+                if 0 <= piece < PIECES:
+                    window_piece(tile_index, piece)
+                if piece == -1:
+                    pad_maps(tile_index)
 
         hidden_grouped = grouped_pool.tile([P, PIXELS, PACK], BF16, align_bytes=64, tag="grouped")
         nc.vector.tensor_copy(out=hidden_grouped[:], in_=hidden[:].rearrange("p t x -> p x t"))

@@ -24,22 +24,21 @@ A = GROUP_CHANNELS // 16
 GROUP_COLUMNS = GROUP_CHANNELS * WINDOW
 TILES = 2 * GROUPS
 
-HALF_SIDE = SIDE // 2
-PITCH = 32
-FIRST = 8
-
 WORDS = 4
-NEIGHBOURS = 8
+WORD_POSITIONS = [[3 * di, 3 * di + 2] for di in range(3)] + [[1, 7]]
+NEIGHBOURS = 2 * WORDS
+
+PITCH = 20
+FIRST = 2
 
 D_TILES = HIDDEN // P
 CHUNKS = GROUPS * D_TILES
-STEPS = 2 * CHUNKS
-SORT_AHEAD = 3
+STEPS = TILES * D_TILES
 W2_CALLS = 4
-FIRST_W2_ITEM = -4
-QUANTISE_W2 = 25
-PIECES = 4
-RAW_AHEAD = 3
+W2_AFTER = [8, 12, 16, 20]
+RAW_AHEAD = 4
+SORT_LEAD = 6
+WINDOW_LEAD = 5
 
 K_GROUPS = CHANNELS // (2 * P)
 
@@ -57,22 +56,14 @@ def tile_localpredictor_pa_k_kernel(tc, z, W1, b1, W2, b2, out):
         keep = ctx.enter_context(tc.tile_pool(name="keep", bufs=1))
         z_pool = ctx.enter_context(tc.tile_pool(name="z", bufs=TILES))
         raw_pool = ctx.enter_context(tc.tile_pool(name="raw", bufs=RAW_AHEAD + 1))
-        window_pool = ctx.enter_context(tc.tile_pool(name="window", bufs=2))
-        win_pool = ctx.enter_context(tc.tile_pool(name="win", bufs=4))
-        sorted_pool = ctx.enter_context(tc.tile_pool(name="sorted", bufs=SORT_AHEAD + 2))
+        win_pool = ctx.enter_context(tc.tile_pool(name="win", bufs=3))
+        sorted_pool = ctx.enter_context(tc.tile_pool(name="sorted", bufs=6))
         grouped_pool = ctx.enter_context(tc.tile_pool(name="grouped", bufs=3))
-        w2_grouped_pool = ctx.enter_context(tc.tile_pool(name="w2_grouped", bufs=W2_CALLS))
         w1q_pool = ctx.enter_context(tc.tile_pool(name="w1q", bufs=3))
         res_pool = ctx.enter_context(tc.tile_pool(name="res", bufs=3))
         turn_pool = ctx.enter_context(tc.psum_pool(name="turn", bufs=4))
         sum_pool = ctx.enter_context(tc.psum_pool(name="sums", bufs=D_TILES))
         ctx.enter_context(tc.manual_schedule())
-
-        ident = keep.tile([P, P], F32)
-        make_identity(nc, ident[:])
-
-        bias_rows = keep.tile([P, 2 * P], BF16)
-        nc.vector.memset(bias_rows[:].bitcast(I32), 0)
 
         first_use = keep.tile([P, 1], F32)
         nc.vector.memset(first_use[:], 0.0)
@@ -96,109 +87,110 @@ def tile_localpredictor_pa_k_kernel(tc, z, W1, b1, W2, b2, out):
             nc.sync.dma_start(out=raw[:], in_=w1_view[u, e, :, GROUP_COLUMNS * group : GROUP_COLUMNS * (group + 1)])
             return raw
 
-        maps = [load_maps(0), load_maps(1)]
+        maps = [load_maps(0)]
+        bias_rows = keep.tile([P, 2 * P], BF16)
+        nc.gpsimd.memset(bias_rows[:].bitcast(I32), 0)
         nc.sync.dma_start(out=bias_rows[0:2, :], in_=b1.rearrange("(u x) -> u x", u=2))
         nc.sync.dma_start(out=bias_rows[2 : 2 + K_GROUPS, :], in_=b2.rearrange("(g x) -> g x", g=K_GROUPS))
+        raws = [load_chunk(0), load_chunk(1)]
+        maps.append(load_maps(1))
+        raws.extend([load_chunk(2), load_chunk(3)])
         w2_raw = keep.tile([P, K_GROUPS, 2, HIDDEN], BF16)
         nc.sync.dma_start(out=w2_raw[:].rearrange("p g e d -> p g (e d)"), in_=w2_view)
-        raws = [load_chunk(chunk) for chunk in range(RAW_AHEAD)]
-        maps = maps + [load_maps(2), load_maps(3)]
+        maps.append(load_maps(2))
 
-        padded_tiles = [keep.tile([P, 2, 2, SIDE + 2, BATCH, PITCH], BF16, name="padded%d" % i) for i in range(2)]
-        nc.vector.memset(padded_tiles[0][:].rearrange("p x j r b c -> p (x j r b c)").bitcast(I32), 0)
-        nc.gpsimd.memset(padded_tiles[1][:].rearrange("p x j r b c -> p (x j r b c)").bitcast(I32), 0)
+        pairs_tiles = [keep.tile([P, SIDE + 2, PITCH, BATCH], F32, name="pairs%d" % i) for i in range(2)]
+        side_tiles = [
+            keep.tile([P, SIDE + 2, SIDE, BATCH, 2], F32, align_bytes=64, name="side%d" % i) for i in range(2)
+        ]
+        updown_tiles = [keep.tile([P, SIDE, SIDE, BATCH, 2], F32, align_bytes=64, name="updown%d" % i) for i in range(2)]
+        for i in range(2):
+            zero = nc.vector.memset if i == 0 else nc.gpsimd.memset
+            zero(pairs_tiles[i][:], 0.0)
+            for row in (0, SIDE + 1):
+                zero(side_tiles[i][:, row], 0.0)
 
-        cross_of = {}
-        ends_of = {}
+        ident = keep.tile([P, P], F32)
+        make_identity(nc, ident[:])
+
+        def make_pairs(tile_index, engine_copy):
+            engine_copy(
+                out=pairs_tiles[tile_index % 2][:, 1 : SIDE + 1, FIRST : FIRST + SIDE, :]
+                .bitcast(BF16)
+                .rearrange("p h w (b j) -> p h w b j", b=BATCH),
+                in_=maps[tile_index][:].rearrange("p b j h w -> p h w b j"),
+            )
+
+        def make_side(tile_index, part, engine_copy):
+            first = FIRST - 1 + 2 * part
+            engine_copy(
+                out=side_tiles[tile_index % 2][:, 1 : SIDE + 1].rearrange(
+                    "p r (q h m) b u -> p h r q m b u", h=2, m=2
+                )[:, part],
+                in_=pairs_tiles[tile_index % 2][:, 1 : SIDE + 1, first : first + SIDE, :].rearrange(
+                    "p r (q u m) b -> p r q m b u", u=2, m=2
+                ),
+            )
+
+        def make_updown(tile_index, part, engine_copy):
+            engine_copy(
+                out=updown_tiles[tile_index % 2][:].rearrange("p (q h m) c b u -> p h q m c b u", h=2, m=2)[:, part],
+                in_=pairs_tiles[tile_index % 2][:, 2 * part : 2 * part + SIDE, FIRST : FIRST + SIDE, :].rearrange(
+                    "p (q u m) c b -> p q m c b u", u=2, m=2
+                ),
+            )
+
         win_of = {}
 
-        def pad_maps(tile_index):
-            padded = padded_tiles[tile_index % 2]
-            by_row = maps[tile_index][:].rearrange("p b j h w -> p j h b w")
-            nc.scalar.copy(out=padded[:, 0, :, 1 : SIDE + 1, :, FIRST : FIRST + SIDE], in_=by_row)
-            nc.scalar.copy(out=padded[:, 1, :, 0:SIDE, :, FIRST + 2 : FIRST + 2 + SIDE], in_=by_row)
-
-        def build_cross(tile_index):
-            cross = window_pool.tile([P, SIDE + 1, BATCH, 2, HALF_SIDE, 2, 2], BF16, align_bytes=64, tag="cross")
-            pairs = padded_tiles[tile_index % 2][:, :, :, 0 : SIDE + 1, :, FIRST + 1 : FIRST + 1 + SIDE].rearrange(
-                "p x j r b (k y) -> p y r b k j x", y=2
-            )
-            for y in range(2):
-                nc.vector.tensor_copy(out=cross[:, :, :, y], in_=pairs[:, y])
-            cross_of[tile_index] = cross
-
-        def build_ends(tile_index, which, engine_copy):
-            if tile_index not in ends_of:
-                ends_of[tile_index] = window_pool.tile(
-                    [P, 2, SIDE, BATCH, 2, HALF_SIDE, 2, 2], BF16, align_bytes=64, tag="ends", name="ends"
-                )
-            ends = ends_of[tile_index]
-            for y in range(2):
-                place = FIRST - 1 + which + y
-                pairs = padded_tiles[tile_index % 2][
-                    :, 0, :, 2 * which : 2 * which + SIDE, :, place : place + SIDE
-                ].rearrange("p j r b (k x) -> p r b k j x", x=2)
-                engine_copy(out=ends[:, which, :, :, y], in_=pairs)
-
-        def quantise_windows(tile_index, words):
+        def quantise_windows(tile_index, word):
             if tile_index not in win_of:
                 codes = win_pool.tile([P, WORDS, PIXELS], U32, align_bytes=64, tag="win_codes", name="win_codes")
                 scales = win_pool.tile([P, WORDS, PIXELS], U8, align_bytes=64, tag="win_scales", name="win_scales")
                 win_of[tile_index] = (codes, scales)
             codes, scales = win_of[tile_index]
-            ends, cross = ends_of[tile_index], cross_of[tile_index]
-            sources = [ends[:, 0], cross[:, 0:SIDE], cross[:, 1 : SIDE + 1], ends[:, 1]]
-            for word in words:
-                nc.vector.quantize_mx(
-                    out=codes[:, word, :].bitcast(FP8X4),
-                    scales=scales[:, word, :],
-                    in_=sources[word].rearrange("p r b y k j x -> p (r b y k j x)"),
-                )
-
-        def window_piece(tile_index, piece):
-            if piece == 0:
-                build_cross(tile_index)
-                build_ends(tile_index, 0, nc.scalar.copy)
-            elif piece == 1:
-                build_ends(tile_index, 1, nc.vector.tensor_copy)
-            elif piece == 2:
-                quantise_windows(tile_index, [1, 2])
+            if word < 3:
+                source = side_tiles[tile_index % 2][:, word : word + SIDE]
             else:
-                quantise_windows(tile_index, [0, 3])
+                source = updown_tiles[tile_index % 2][:]
+            nc.vector.quantize_mx(
+                out=codes[:, word, :].bitcast(FP8X4),
+                scales=scales[:, word, :],
+                in_=source.rearrange("p r c b u -> p (r c b u)").bitcast(BF16),
+            )
 
         ordered_tiles = {}
 
-        def sort_step(step):
-            chunk, half = divmod(step, 2)
+        def sort_runs(chunk, side_of_centre, halves, engine_copy):
+            if chunk not in ordered_tiles:
+                ordered_tiles[chunk] = sorted_pool.tile([P, 2, NEIGHBOURS, 2 * P], BF16, tag="ordered", name="ordered")
             by_channel = raws[chunk][:].rearrange("d (a s e c k) -> d s e a c k", a=A, s=2, e=2, c=4, k=WINDOW)
-            ordered = sorted_pool.tile([P, NEIGHBOURS, 2 * P], BF16, tag="ordered")
-            for side in range(2):
-                runs = by_channel[:, half, :, :, :, 5 * side : 5 * side + 4]
-                planes = ordered[:, 4 * side : 4 * side + 4, :]
-                engine_copy = nc.scalar.copy if side == 1 and half == 1 else nc.vector.tensor_copy
-                engine_copy(
-                    out=planes.rearrange("d (j g) (e a r x) -> d e a r j g x", j=2, e=2, a=A, r=2),
-                    in_=runs.rearrange("d e a (r j) (g x) -> d e a r j g x", r=2, g=2),
-                )
-            ordered_tiles[step] = ordered
+            first = 4 * side_of_centre
+            engine_copy(
+                out=ordered_tiles[chunk][:, halves, first : first + 4, :].rearrange(
+                    "d s k (e a c) -> d s e a c k", e=2, c=4
+                ),
+                in_=by_channel[:, halves, :, :, :, first + side_of_centre : first + side_of_centre + 4],
+            )
 
         w2_codes = keep.tile([P, 2 * K_GROUPS * P], U32, align_bytes=64)
         w2_scales = keep.tile([P, 2 * K_GROUPS * P], U8, align_bytes=64)
+        neighbour_of = [position - (position > WINDOW // 2) for pair in WORD_POSITIONS for position in pair]
 
-        def is_item(item):
-            return FIRST_W2_ITEM <= item < FIRST_W2_ITEM + W2_CALLS or 0 <= item < STEPS
+        items = []
+        for step in range(STEPS):
+            items.append(("W1", step))
+            if step in W2_AFTER:
+                items.append(("W2", W2_AFTER.index(step)))
+        place_of_step = [items.index(("W1", step)) for step in range(STEPS)]
 
         def planes_of(item):
-            if item >= 0:
-                return [
-                    ordered_tiles[item][:, 4 * s + 2 * j + g, :].bitcast(F32)
-                    for s in range(2)
-                    for g in range(2)
-                    for j in range(2)
-                ]
-            call = item - FIRST_W2_ITEM
+            kind, index = item
+            if kind == "W1":
+                tile_index, d_tile = divmod(index, D_TILES)
+                group, half = divmod(tile_index, 2)
+                return [ordered_tiles[D_TILES * group + d_tile][:, half, n, :].bitcast(F32) for n in neighbour_of]
             return [
-                w2_raw[:, 2 * call + g, e, 2 * P * u : 2 * P * (u + 1)].bitcast(F32)
+                w2_raw[:, 2 * index + g, e, 2 * P * u : 2 * P * (u + 1)].bitcast(F32)
                 for g in range(2)
                 for e in range(2)
                 for u in range(2)
@@ -218,8 +210,7 @@ def tile_localpredictor_pa_k_kernel(tc, z, W1, b1, W2, b2, out):
                 turned_tiles[item].append(turned)
 
         def drain(item):
-            pool = grouped_pool if item >= 0 else w2_grouped_pool
-            grouped = pool.tile([P, 2, 2, P, PACK], BF16, align_bytes=64, tag="grouped")
+            grouped = grouped_pool.tile([P, 2, 2, P, PACK], BF16, align_bytes=64, tag="grouped")
             for bank in range(2):
                 nc.scalar.copy(
                     out=grouped[:, bank].bitcast(F32),
@@ -228,12 +219,13 @@ def tile_localpredictor_pa_k_kernel(tc, z, W1, b1, W2, b2, out):
             grouped_tiles[item] = grouped
 
         def quantise(item):
-            if item >= 0:
+            kind, index = item
+            if kind == "W1":
                 codes = w1q_pool.tile([P, WORDS * P], U32, align_bytes=64, tag="w1_codes")
                 scales = w1q_pool.tile([P, WORDS * P], U8, align_bytes=64, tag="w1_scales")
                 codes_of[item] = (codes[:], scales[:])
             else:
-                columns = slice(WORDS * P * (item - FIRST_W2_ITEM), WORDS * P * (item - FIRST_W2_ITEM + 1))
+                columns = slice(WORDS * P * index, WORDS * P * (index + 1))
                 codes_of[item] = (w2_codes[:, columns], w2_scales[:, columns])
             nc.vector.quantize_mx(
                 out=codes_of[item][0].bitcast(FP8X4),
@@ -245,10 +237,9 @@ def tile_localpredictor_pa_k_kernel(tc, z, W1, b1, W2, b2, out):
         hidden = keep.tile([P, D_TILES, PIXELS], BF16)
 
         def multiply(step):
-            chunk, half = divmod(step, 2)
-            group, d_tile = divmod(chunk, D_TILES)
-            codes, scales = codes_of[step]
-            win_codes, win_scales = win_of[2 * group + half]
+            tile_index, d_tile = divmod(step, D_TILES)
+            codes, scales = codes_of[("W1", step)]
+            win_codes, win_scales = win_of[tile_index]
             for word in range(WORDS):
                 rows = slice(P * word, P * (word + 1))
                 nc.tensor.matmul_mx(
@@ -257,55 +248,93 @@ def tile_localpredictor_pa_k_kernel(tc, z, W1, b1, W2, b2, out):
                     lhsT_scale=scales[:, rows],
                     rhs=win_codes[:, word, :].bitcast(FP8X4),
                     rhs_scale=win_scales[:, word, :],
-                    start=(group == 0 and half == 0 and word == 0),
-                    stop=(group == GROUPS - 1 and half == 1 and word == WORDS - 1),
+                    start=(tile_index == 0 and word == 0),
+                    stop=(tile_index == TILES - 1 and word == WORDS - 1),
                 )
 
-        bias_turned = turn_pool.tile([P, 4, P], F32, tag="turned")
-        nc.tensor.transpose(bias_turned[:, 0, :], bias_rows[:].bitcast(F32), ident[:])
         bias = keep.tile([P, 2 * (2 + K_GROUPS)], F32)
 
-        def first_window_tick(tile_index):
-            return PIECES * (tile_index - 2) + 1
+        def make_bias():
+            bias_turned = turn_pool.tile([P, 4, P], F32, tag="turned")
+            nc.tensor.transpose(bias_turned[:, 0, :], bias_rows[:].bitcast(F32), ident[:])
+            nc.vector.tensor_copy(out=bias[:], in_=bias_turned[:, 0, 0 : 2 + K_GROUPS].bitcast(BF16))
 
-        for t in range(-PIECES * 2 - 1, STEPS + 3):
-            if is_item(t + 1):
-                turn(t + 1)
-            if is_item(t):
-                drain(t)
-            if 0 <= t - 1 < STEPS:
-                quantise(t - 1)
-            if 0 <= t - 2 < STEPS:
-                multiply(t - 2)
-            finished_chunk, last = divmod(t - 3, 2)
-            if last == 1 and CHUNKS - D_TILES <= finished_chunk < CHUNKS:
-                d_tile = finished_chunk % D_TILES
-                for b in range(BATCH):
-                    nc.scalar.activation(
-                        out=hidden[:, d_tile, IMAGE * b : IMAGE * (b + 1)].rearrange("p (r k y) -> p r k y", r=SIDE, y=2),
-                        in_=sums[d_tile][:].rearrange("p (r b y k) -> p b r k y", r=SIDE, b=BATCH, y=2)[:, b],
-                        func=ACT.Relu,
-                        bias=bias[:, d_tile : d_tile + 1],
-                        scale=1.0,
-                    )
-            if 0 <= t + SORT_AHEAD < STEPS:
-                chunk, half = divmod(t + SORT_AHEAD, 2)
-                if half == 0 and 1 <= chunk and chunk + RAW_AHEAD - 1 < CHUNKS:
-                    raws.append(load_chunk(chunk + RAW_AHEAD - 1))
-                    next_tile = 2 * (chunk // D_TILES) + 4
-                    if chunk % D_TILES == 1 and next_tile < TILES:
-                        maps = maps + [load_maps(next_tile), load_maps(next_tile + 1)]
-                sort_step(t + SORT_AHEAD)
-            if t == FIRST_W2_ITEM:
-                nc.vector.tensor_copy(out=bias[:], in_=bias_turned[:, 0, 0 : 2 + K_GROUPS].bitcast(BF16))
-            if 0 <= t - QUANTISE_W2 < W2_CALLS:
-                quantise(FIRST_W2_ITEM + t - QUANTISE_W2)
-            for tile_index in range(TILES):
-                piece = t - first_window_tick(tile_index)
-                if 0 <= piece < PIECES:
-                    window_piece(tile_index, piece)
-                if piece == -1:
-                    pad_maps(tile_index)
+        jobs = {}
+
+        def at(tick, job):
+            jobs.setdefault(tick, []).append(job)
+
+        def tick_of(step):
+            return place_of_step[step] if step >= 0 else step
+
+        FIRST_TICK = -SORT_LEAD
+
+        def window_jobs(tile_index):
+            copy = nc.vector.tensor_copy if tile_index == 0 else nc.scalar.copy
+            make = [
+                lambda: make_pairs(tile_index, copy),
+                lambda: (make_side(tile_index, 0, copy), make_side(tile_index, 1, copy)),
+                lambda: (make_updown(tile_index, 0, copy), make_updown(tile_index, 1, copy)),
+            ]
+            words = [lambda word=word: quantise_windows(tile_index, word) for word in range(WORDS)]
+            return make, words
+
+        make, words = window_jobs(0)
+        for job in make + words[:2]:
+            at(FIRST_TICK, job)
+        at(FIRST_TICK, make_bias)
+        at(FIRST_TICK + 2, words[2])
+        at(FIRST_TICK + 4, words[3])
+        for tile_index in range(1, TILES):
+            start = tick_of(D_TILES * tile_index) - WINDOW_LEAD
+            make, words = window_jobs(tile_index)
+            for offset, job in [(0, make[0]), (1, make[1]), (3, make[2])]:
+                at(start + offset, job)
+            for word in range(WORDS):
+                at(start + 2 + word, words[word])
+
+        def sort_jobs(chunk):
+            shared = chunk % 2 == 1
+
+            def before_centre():
+                sort_runs(chunk, 0, slice(0, 2), nc.vector.tensor_copy)
+
+            def behind_centre():
+                sort_runs(chunk, 1, slice(0, 1) if shared else slice(0, 2), nc.vector.tensor_copy)
+                if shared:
+                    sort_runs(chunk, 1, slice(1, 2), nc.scalar.copy)
+                    if len(maps) < TILES:
+                        maps.append(load_maps(len(maps)))
+                if chunk + RAW_AHEAD < CHUNKS:
+                    raws.append(load_chunk(chunk + RAW_AHEAD))
+
+            return before_centre, behind_centre
+
+        for chunk in range(CHUNKS):
+            before_centre, behind_centre = sort_jobs(chunk)
+            at(tick_of(2 * chunk - SORT_LEAD), before_centre)
+            at(tick_of(2 * chunk - SORT_LEAD + 1), behind_centre)
+
+        for n in range(FIRST_TICK, len(items) + 3):
+            if 0 <= n + 1 < len(items):
+                turn(items[n + 1])
+            if 0 <= n < len(items):
+                drain(items[n])
+            if 0 <= n - 1 < len(items):
+                quantise(items[n - 1])
+            if 0 <= n - 2 < len(items) and items[n - 2][0] == "W1":
+                multiply(items[n - 2][1])
+            if 0 <= n - 3 < len(items) and items[n - 3][1] >= STEPS - D_TILES:
+                d_tile = items[n - 3][1] % D_TILES
+                nc.scalar.activation(
+                    out=hidden[:, d_tile, :].rearrange("p (b x) -> p b x", b=BATCH),
+                    in_=sums[d_tile][:].rearrange("p (x b) -> p b x", b=BATCH),
+                    func=ACT.Relu,
+                    bias=bias[:, d_tile : d_tile + 1],
+                    scale=1.0,
+                )
+            for job in jobs.get(n, []):
+                job()
 
         hidden_grouped = grouped_pool.tile([P, PIXELS, PACK], BF16, align_bytes=64, tag="grouped")
         nc.vector.tensor_copy(out=hidden_grouped[:], in_=hidden[:].rearrange("p t x -> p x t"))

@@ -36,9 +36,10 @@ CHUNKS = GROUPS * D_TILES
 STEPS = TILES * D_TILES
 W2_CALLS = 4
 W2_AFTER = [8, 12, 16, 20]
-RAW_AHEAD = 4
-SORT_LEAD = 6
-WINDOW_LEAD = 5
+RAW_AHEAD = 6
+W2_LOAD = 3
+SORT_LEAD = 3
+WINDOW_LEAD = 6
 
 K_GROUPS = CHANNELS // (2 * P)
 
@@ -55,12 +56,12 @@ def tile_localpredictor_pa_k_kernel(tc, z, W1, b1, W2, b2, out):
     with ExitStack() as ctx:
         keep = ctx.enter_context(tc.tile_pool(name="keep", bufs=1))
         z_pool = ctx.enter_context(tc.tile_pool(name="z", bufs=TILES))
-        raw_pool = ctx.enter_context(tc.tile_pool(name="raw", bufs=RAW_AHEAD + 1))
+        raw_pool = ctx.enter_context(tc.tile_pool(name="raw", bufs=RAW_AHEAD))
         win_pool = ctx.enter_context(tc.tile_pool(name="win", bufs=3))
-        sorted_pool = ctx.enter_context(tc.tile_pool(name="sorted", bufs=6))
+        sorted_pool = ctx.enter_context(tc.tile_pool(name="sorted", bufs=SORT_LEAD + 2))
         grouped_pool = ctx.enter_context(tc.tile_pool(name="grouped", bufs=3))
         w1q_pool = ctx.enter_context(tc.tile_pool(name="w1q", bufs=3))
-        res_pool = ctx.enter_context(tc.tile_pool(name="res", bufs=3))
+        res_pool = ctx.enter_context(tc.tile_pool(name="res", bufs=6))
         turn_pool = ctx.enter_context(tc.psum_pool(name="turn", bufs=4))
         sum_pool = ctx.enter_context(tc.psum_pool(name="sums", bufs=D_TILES))
         ctx.enter_context(tc.manual_schedule())
@@ -95,9 +96,9 @@ def tile_localpredictor_pa_k_kernel(tc, z, W1, b1, W2, b2, out):
         raws = [load_chunk(0), load_chunk(1)]
         maps.append(load_maps(1))
         raws.extend([load_chunk(2), load_chunk(3)])
-        w2_raw = keep.tile([P, K_GROUPS, 2, HIDDEN], BF16)
-        nc.sync.dma_start(out=w2_raw[:].rearrange("p g e d -> p g (e d)"), in_=w2_view)
         maps.append(load_maps(2))
+        raws.extend([load_chunk(4), load_chunk(5)])
+        w2_raw = keep.tile([P, K_GROUPS, 2, HIDDEN], BF16)
 
         pairs_tiles = [keep.tile([P, SIDE + 2, PITCH, BATCH], F32, name="pairs%d" % i) for i in range(2)]
         side_tiles = [
@@ -160,17 +161,23 @@ def tile_localpredictor_pa_k_kernel(tc, z, W1, b1, W2, b2, out):
 
         ordered_tiles = {}
 
-        def sort_runs(chunk, side_of_centre, halves, engine_copy):
-            if chunk not in ordered_tiles:
-                ordered_tiles[chunk] = sorted_pool.tile([P, 2, NEIGHBOURS, 2 * P], BF16, tag="ordered", name="ordered")
-            by_channel = raws[chunk][:].rearrange("d (a s e c k) -> d s e a c k", a=A, s=2, e=2, c=4, k=WINDOW)
-            first = 4 * side_of_centre
-            engine_copy(
-                out=ordered_tiles[chunk][:, halves, first : first + 4, :].rearrange(
-                    "d s k (e a c) -> d s e a c k", e=2, c=4
-                ),
-                in_=by_channel[:, halves, :, :, :, first + side_of_centre : first + side_of_centre + 4],
-            )
+        def chunk_of(step):
+            tile_index, d_tile = divmod(step, D_TILES)
+            return D_TILES * (tile_index // 2) + d_tile
+
+        def sort_step(step):
+            half = step // D_TILES % 2
+            by_channel = raws[chunk_of(step)][:].rearrange("d (a s e c k) -> d s e a c k", a=A, s=2, e=2, c=4, k=WINDOW)
+            ordered = sorted_pool.tile([P, NEIGHBOURS, 2 * P], BF16, tag="ordered")
+            for side_of_centre in range(2):
+                first = 4 * side_of_centre
+                on_scalar = side_of_centre == 1 and step > D_TILES and step % D_TILES == D_TILES - 1
+                engine_copy = nc.scalar.copy if on_scalar else nc.vector.tensor_copy
+                engine_copy(
+                    out=ordered[:, first : first + 4, :].rearrange("d k (e a c) -> d e a c k", e=2, c=4),
+                    in_=by_channel[:, half, :, :, :, first + side_of_centre : first + side_of_centre + 4],
+                )
+            ordered_tiles[step] = ordered
 
         w2_codes = keep.tile([P, 2 * K_GROUPS * P], U32, align_bytes=64)
         w2_scales = keep.tile([P, 2 * K_GROUPS * P], U8, align_bytes=64)
@@ -186,9 +193,7 @@ def tile_localpredictor_pa_k_kernel(tc, z, W1, b1, W2, b2, out):
         def planes_of(item):
             kind, index = item
             if kind == "W1":
-                tile_index, d_tile = divmod(index, D_TILES)
-                group, half = divmod(tile_index, 2)
-                return [ordered_tiles[D_TILES * group + d_tile][:, half, n, :].bitcast(F32) for n in neighbour_of]
+                return [ordered_tiles[index][:, n, :].bitcast(F32) for n in neighbour_of]
             return [
                 w2_raw[:, 2 * index + g, e, 2 * P * u : 2 * P * (u + 1)].bitcast(F32)
                 for g in range(2)
@@ -234,7 +239,17 @@ def tile_localpredictor_pa_k_kernel(tc, z, W1, b1, W2, b2, out):
             )
 
         sums = [sum_pool.tile([P, PIXELS], F32, tag="sums", name="hidden_sums%d" % i) for i in range(D_TILES)]
-        hidden = keep.tile([P, D_TILES, PIXELS], BF16)
+        hidden = keep.tile([P, D_TILES, BATCH, IMAGE], BF16)
+
+        def relu(d_tile):
+            for b in range(BATCH):
+                nc.scalar.activation(
+                    out=hidden[:, d_tile, b, :],
+                    in_=sums[d_tile][:].rearrange("p (x b) -> p b x", b=BATCH)[:, b],
+                    func=ACT.Relu,
+                    bias=bias[:, d_tile : d_tile + 1],
+                    scale=1.0,
+                )
 
         def multiply(step):
             tile_index, d_tile = divmod(step, D_TILES)
@@ -267,7 +282,7 @@ def tile_localpredictor_pa_k_kernel(tc, z, W1, b1, W2, b2, out):
         def tick_of(step):
             return place_of_step[step] if step >= 0 else step
 
-        FIRST_TICK = -SORT_LEAD
+        FIRST_TICK = -SORT_LEAD - 1
 
         def window_jobs(tile_index):
             copy = nc.vector.tensor_copy if tile_index == 0 else nc.scalar.copy
@@ -280,40 +295,32 @@ def tile_localpredictor_pa_k_kernel(tc, z, W1, b1, W2, b2, out):
             return make, words
 
         make, words = window_jobs(0)
-        for job in make + words[:2]:
+        for job in [make[0], make[1], words[0], make[2], words[1], words[2], words[3]]:
             at(FIRST_TICK, job)
         at(FIRST_TICK, make_bias)
-        at(FIRST_TICK + 2, words[2])
-        at(FIRST_TICK + 4, words[3])
         for tile_index in range(1, TILES):
             start = tick_of(D_TILES * tile_index) - WINDOW_LEAD
             make, words = window_jobs(tile_index)
-            for offset, job in [(0, make[0]), (1, make[1]), (3, make[2])]:
+            for offset, job in [(0, make[0]), (1, make[1]), (2, make[2])]:
                 at(start + offset, job)
             for word in range(WORDS):
                 at(start + 2 + word, words[word])
 
-        def sort_jobs(chunk):
-            shared = chunk % 2 == 1
+        def sort_job(step):
+            def work():
+                sort_step(step)
+                chunk = chunk_of(step) + RAW_AHEAD
+                if step // D_TILES % 2 == 1 and chunk < CHUNKS:
+                    raws.append(load_chunk(chunk))
+                if step == W2_LOAD:
+                    nc.sync.dma_start(out=w2_raw[:].rearrange("p g e d -> p g (e d)"), in_=w2_view)
+                if step % D_TILES == 0 and len(maps) < TILES:
+                    maps.append(load_maps(len(maps)))
 
-            def before_centre():
-                sort_runs(chunk, 0, slice(0, 2), nc.vector.tensor_copy)
+            return work
 
-            def behind_centre():
-                sort_runs(chunk, 1, slice(0, 1) if shared else slice(0, 2), nc.vector.tensor_copy)
-                if shared:
-                    sort_runs(chunk, 1, slice(1, 2), nc.scalar.copy)
-                    if len(maps) < TILES:
-                        maps.append(load_maps(len(maps)))
-                if chunk + RAW_AHEAD < CHUNKS:
-                    raws.append(load_chunk(chunk + RAW_AHEAD))
-
-            return before_centre, behind_centre
-
-        for chunk in range(CHUNKS):
-            before_centre, behind_centre = sort_jobs(chunk)
-            at(tick_of(2 * chunk - SORT_LEAD), before_centre)
-            at(tick_of(2 * chunk - SORT_LEAD + 1), behind_centre)
+        for step in range(STEPS):
+            at(tick_of(step - SORT_LEAD), sort_job(step))
 
         for n in range(FIRST_TICK, len(items) + 3):
             if 0 <= n + 1 < len(items):
@@ -325,46 +332,41 @@ def tile_localpredictor_pa_k_kernel(tc, z, W1, b1, W2, b2, out):
             if 0 <= n - 2 < len(items) and items[n - 2][0] == "W1":
                 multiply(items[n - 2][1])
             if 0 <= n - 3 < len(items) and items[n - 3][1] >= STEPS - D_TILES:
-                d_tile = items[n - 3][1] % D_TILES
-                nc.scalar.activation(
-                    out=hidden[:, d_tile, :].rearrange("p (b x) -> p b x", b=BATCH),
-                    in_=sums[d_tile][:].rearrange("p (x b) -> p b x", b=BATCH),
-                    func=ACT.Relu,
-                    bias=bias[:, d_tile : d_tile + 1],
-                    scale=1.0,
-                )
+                relu(items[n - 3][1] % D_TILES)
             for job in jobs.get(n, []):
                 job()
 
-        hidden_grouped = grouped_pool.tile([P, PIXELS, PACK], BF16, align_bytes=64, tag="grouped")
-        nc.vector.tensor_copy(out=hidden_grouped[:], in_=hidden[:].rearrange("p t x -> p x t"))
-        hidden_codes = keep.tile([P, PIXELS], U32, align_bytes=64)
-        hidden_scales = keep.tile([P, PIXELS], U8, align_bytes=64)
-        nc.vector.quantize_mx(
-            out=hidden_codes[:].bitcast(FP8X4),
-            scales=hidden_scales[:],
-            in_=hidden_grouped[:].rearrange("p x t -> p (x t)"),
-        )
-
-        for g in range(K_GROUPS):
-            res = res_pool.tile([P, BATCH, 2, IMAGE], F32, tag="res")
-            for e in range(2):
-                k_tile = 2 * g + e
-                rows = slice(P * k_tile, P * (k_tile + 1))
-                logits = sum_pool.tile([P, PIXELS], F32, tag="sums")
-                nc.tensor.matmul_mx(
-                    out=logits[:],
-                    lhsT=w2_codes[:, rows].bitcast(FP8X4),
-                    lhsT_scale=w2_scales[:, rows],
-                    rhs=hidden_codes[:].bitcast(FP8X4),
-                    rhs_scale=hidden_scales[:],
-                    start=True,
-                    stop=True,
-                )
-                by_image = logits[:].rearrange("p (b x) -> p b x", b=BATCH)
-                b2_column = bias[:, 4 + k_tile : 5 + k_tile]
-                if e == 0:
-                    nc.scalar.activation(out=res[:, :, e, :], in_=by_image, func=ACT.Identity, bias=b2_column, scale=1.0)
-                else:
-                    nc.vector.tensor_scalar_add(out=res[:, :, e, :], in0=by_image, scalar1=b2_column)
-            nc.sync.dma_start(out=out_view[g], in_=res[:].rearrange("p b e x -> p b (e x)"))
+        hidden_codes = keep.tile([P, BATCH, IMAGE], U32, align_bytes=64)
+        hidden_scales = keep.tile([P, BATCH, IMAGE], U8, align_bytes=64)
+        hidden_grouped = keep.tile([P, BATCH, IMAGE, PACK], BF16, align_bytes=64)
+        for b in range(BATCH):
+            engine_copy = nc.vector.tensor_copy if b == 0 else nc.scalar.copy
+            engine_copy(out=hidden_grouped[:, b], in_=hidden[:, :, b, :].rearrange("p t x -> p x t"))
+        for b in range(BATCH):
+            nc.vector.quantize_mx(
+                out=hidden_codes[:, b].bitcast(FP8X4),
+                scales=hidden_scales[:, b],
+                in_=hidden_grouped[:, b].rearrange("p x t -> p (x t)"),
+            )
+        for b in range(BATCH):
+            for g in range(K_GROUPS):
+                logits = sum_pool.tile([P, 2, IMAGE], F32, tag="sums")
+                res = res_pool.tile([P, 2, IMAGE], F32, tag="res")
+                for e in range(2):
+                    rows = slice(P * (2 * g + e), P * (2 * g + e + 1))
+                    nc.tensor.matmul_mx(
+                        out=logits[:, e],
+                        lhsT=w2_codes[:, rows].bitcast(FP8X4),
+                        lhsT_scale=w2_scales[:, rows],
+                        rhs=hidden_codes[:, b].bitcast(FP8X4),
+                        rhs_scale=hidden_scales[:, b],
+                        start=True,
+                        stop=True,
+                    )
+                for e in range(2):
+                    b2_column = bias[:, 4 + 2 * g + e : 5 + 2 * g + e]
+                    if g % 2 == 0:
+                        nc.scalar.activation(out=res[:, e], in_=logits[:, e], func=ACT.Identity, bias=b2_column, scale=1.0)
+                    else:
+                        nc.vector.tensor_scalar_add(out=res[:, e], in0=logits[:, e], scalar1=b2_column)
+                nc.sync.dma_start(out=out_view[g, :, b], in_=res[:].rearrange("p e x -> p (e x)"))

@@ -35,11 +35,12 @@ D_TILES = HIDDEN // P
 CHUNKS = GROUPS * D_TILES
 STEPS = TILES * D_TILES
 W2_CALLS = 4
-W2_AFTER = [8, 12, 16, 20]
-RAW_AHEAD = 6
-W2_LOAD = 3
+W2_AFTER = [18, 21, 24, 27]
+RAW_AHEAD = 5
+W2_LOAD = 7
+MAPS_LOAD = 0
 SORT_LEAD = 3
-WINDOW_LEAD = 6
+WINDOW_LEAD = 7
 
 K_GROUPS = CHANNELS // (2 * P)
 
@@ -57,7 +58,7 @@ def tile_localpredictor_pa_k_kernel(tc, z, W1, b1, W2, b2, out):
         keep = ctx.enter_context(tc.tile_pool(name="keep", bufs=1))
         z_pool = ctx.enter_context(tc.tile_pool(name="z", bufs=TILES))
         raw_pool = ctx.enter_context(tc.tile_pool(name="raw", bufs=RAW_AHEAD))
-        win_pool = ctx.enter_context(tc.tile_pool(name="win", bufs=3))
+        win_pool = ctx.enter_context(tc.tile_pool(name="win", bufs=4))
         sorted_pool = ctx.enter_context(tc.tile_pool(name="sorted", bufs=SORT_LEAD + 2))
         grouped_pool = ctx.enter_context(tc.tile_pool(name="grouped", bufs=3))
         w1q_pool = ctx.enter_context(tc.tile_pool(name="w1q", bufs=3))
@@ -88,16 +89,14 @@ def tile_localpredictor_pa_k_kernel(tc, z, W1, b1, W2, b2, out):
             nc.sync.dma_start(out=raw[:], in_=w1_view[u, e, :, GROUP_COLUMNS * group : GROUP_COLUMNS * (group + 1)])
             return raw
 
-        maps = [load_maps(0)]
+        maps = [load_maps(0), load_maps(1)]
         bias_rows = keep.tile([P, 2 * P], BF16)
         nc.gpsimd.memset(bias_rows[:].bitcast(I32), 0)
         nc.sync.dma_start(out=bias_rows[0:2, :], in_=b1.rearrange("(u x) -> u x", u=2))
         nc.sync.dma_start(out=bias_rows[2 : 2 + K_GROUPS, :], in_=b2.rearrange("(g x) -> g x", g=K_GROUPS))
         raws = [load_chunk(0), load_chunk(1)]
-        maps.append(load_maps(1))
-        raws.extend([load_chunk(2), load_chunk(3)])
         maps.append(load_maps(2))
-        raws.extend([load_chunk(4), load_chunk(5)])
+        raws.extend([load_chunk(chunk) for chunk in range(2, RAW_AHEAD)])
         w2_raw = keep.tile([P, K_GROUPS, 2, HIDDEN], BF16)
 
         pairs_tiles = [keep.tile([P, SIDE + 2, PITCH, BATCH], F32, name="pairs%d" % i) for i in range(2)]
@@ -159,19 +158,21 @@ def tile_localpredictor_pa_k_kernel(tc, z, W1, b1, W2, b2, out):
                 in_=source.rearrange("p r c b u -> p (r c b u)").bitcast(BF16),
             )
 
+        steps = [(tile_index, d_tile) for d_tile in range(D_TILES) for tile_index in range(2)]
+        steps.extend([(tile_index, d_tile) for tile_index in range(2, TILES) for d_tile in range(D_TILES)])
         ordered_tiles = {}
 
         def chunk_of(step):
-            tile_index, d_tile = divmod(step, D_TILES)
+            tile_index, d_tile = steps[step]
             return D_TILES * (tile_index // 2) + d_tile
 
         def sort_step(step):
-            half = step // D_TILES % 2
+            half = steps[step][0] % 2
             by_channel = raws[chunk_of(step)][:].rearrange("d (a s e c k) -> d s e a c k", a=A, s=2, e=2, c=4, k=WINDOW)
             ordered = sorted_pool.tile([P, NEIGHBOURS, 2 * P], BF16, tag="ordered")
             for side_of_centre in range(2):
                 first = 4 * side_of_centre
-                on_scalar = side_of_centre == 1 and step > D_TILES and step % D_TILES == D_TILES - 1
+                on_scalar = side_of_centre == 1 and step % D_TILES == 1 and D_TILES < step < STEPS - D_TILES
                 engine_copy = nc.scalar.copy if on_scalar else nc.vector.tensor_copy
                 engine_copy(
                     out=ordered[:, first : first + 4, :].rearrange("d k (e a c) -> d e a c k", e=2, c=4),
@@ -252,7 +253,7 @@ def tile_localpredictor_pa_k_kernel(tc, z, W1, b1, W2, b2, out):
                 )
 
         def multiply(step):
-            tile_index, d_tile = divmod(step, D_TILES)
+            tile_index, d_tile = steps[step]
             codes, scales = codes_of[("W1", step)]
             win_codes, win_scales = win_of[tile_index]
             for word in range(WORDS):
@@ -299,7 +300,8 @@ def tile_localpredictor_pa_k_kernel(tc, z, W1, b1, W2, b2, out):
             at(FIRST_TICK, job)
         at(FIRST_TICK, make_bias)
         for tile_index in range(1, TILES):
-            start = tick_of(D_TILES * tile_index) - WINDOW_LEAD
+            first_step = min(step for step in range(STEPS) if steps[step][0] == tile_index)
+            start = max(tick_of(first_step - WINDOW_LEAD), FIRST_TICK)
             make, words = window_jobs(tile_index)
             for offset, job in [(0, make[0]), (1, make[1]), (2, make[2])]:
                 at(start + offset, job)
@@ -310,11 +312,11 @@ def tile_localpredictor_pa_k_kernel(tc, z, W1, b1, W2, b2, out):
             def work():
                 sort_step(step)
                 chunk = chunk_of(step) + RAW_AHEAD
-                if step // D_TILES % 2 == 1 and chunk < CHUNKS:
+                if steps[step][0] % 2 == 1 and chunk < CHUNKS:
                     raws.append(load_chunk(chunk))
                 if step == W2_LOAD:
                     nc.sync.dma_start(out=w2_raw[:].rearrange("p g e d -> p g (e d)"), in_=w2_view)
-                if step % D_TILES == 0 and len(maps) < TILES:
+                if step % D_TILES == MAPS_LOAD and len(maps) < TILES:
                     maps.append(load_maps(len(maps)))
 
             return work
@@ -332,7 +334,7 @@ def tile_localpredictor_pa_k_kernel(tc, z, W1, b1, W2, b2, out):
             if 0 <= n - 2 < len(items) and items[n - 2][0] == "W1":
                 multiply(items[n - 2][1])
             if 0 <= n - 3 < len(items) and items[n - 3][1] >= STEPS - D_TILES:
-                relu(items[n - 3][1] % D_TILES)
+                relu(steps[items[n - 3][1]][1])
             for job in jobs.get(n, []):
                 job()
 

@@ -35,9 +35,10 @@ D_TILES = HIDDEN // P
 CHUNKS = GROUPS * D_TILES
 STEPS = TILES * D_TILES
 W2_CALLS = 4
-W2_AFTER = [18, 21, 24, 27]
+W2_AFTER = [14, 18, 22, 26]
 RAW_AHEAD = 5
 W2_LOAD = 7
+SCALAR_SORTS = list(range(5, 24, 4)) + [25, 27, 29]
 MAPS_LOAD = 0
 SORT_LEAD = 3
 WINDOW_LEAD = 7
@@ -172,7 +173,7 @@ def tile_localpredictor_pa_k_kernel(tc, z, W1, b1, W2, b2, out):
             ordered = sorted_pool.tile([P, NEIGHBOURS, 2 * P], BF16, tag="ordered")
             for side_of_centre in range(2):
                 first = 4 * side_of_centre
-                on_scalar = side_of_centre == 1 and step % D_TILES == 1 and D_TILES < step < STEPS - D_TILES
+                on_scalar = side_of_centre == 1 and step in SCALAR_SORTS
                 engine_copy = nc.scalar.copy if on_scalar else nc.vector.tensor_copy
                 engine_copy(
                     out=ordered[:, first : first + 4, :].rearrange("d k (e a c) -> d e a c k", e=2, c=4),
@@ -243,10 +244,11 @@ def tile_localpredictor_pa_k_kernel(tc, z, W1, b1, W2, b2, out):
         hidden = keep.tile([P, D_TILES, BATCH, IMAGE], BF16)
 
         def relu(d_tile):
-            for b in range(BATCH):
+            images = [slice(0, BATCH)] if d_tile < D_TILES - 1 else [slice(b, b + 1) for b in range(BATCH)]
+            for image in images:
                 nc.scalar.activation(
-                    out=hidden[:, d_tile, b, :],
-                    in_=sums[d_tile][:].rearrange("p (x b) -> p b x", b=BATCH)[:, b],
+                    out=hidden[:, d_tile, image, :],
+                    in_=sums[d_tile][:].rearrange("p (x b) -> p b x", b=BATCH)[:, image],
                     func=ACT.Relu,
                     bias=bias[:, d_tile : d_tile + 1],
                     scale=1.0,

@@ -18,11 +18,10 @@ WINDOW = 9
 IMAGE = SIDE * SIDE
 PIXELS = BATCH * IMAGE
 
-GROUPS = 4
-GROUP_CHANNELS = CHANNELS // GROUPS
-A = GROUP_CHANNELS // 16
-GROUP_COLUMNS = GROUP_CHANNELS * WINDOW
-TILES = 2 * GROUPS
+TILES = 8
+TILE_CHANNELS = CHANNELS // TILES
+A = TILE_CHANNELS // 16
+TILE_COLUMNS = TILE_CHANNELS * WINDOW
 
 WORDS = 4
 WORD_POSITIONS = [[3 * di, 3 * di + 2] for di in range(3)] + [[1, 7]]
@@ -32,16 +31,15 @@ PITCH = 20
 FIRST = 2
 
 D_TILES = HIDDEN // P
-CHUNKS = GROUPS * D_TILES
 STEPS = TILES * D_TILES
 W2_CALLS = 4
 W2_AFTER = [14, 18, 22, 26]
-RAW_AHEAD = 5
+RAW_AHEAD = 10
 W2_LOAD = 7
-SCALAR_SORTS = list(range(5, 24, 4)) + [25, 27, 29]
-MAPS_LOAD = 0
+PERMUTE_AFTER = [1, 9, 17]
+SCALAR_SORTS = list(range(6, 31, 3))
 SORT_LEAD = 3
-WINDOW_LEAD = 7
+WINDOW_LEAD = 5
 
 K_GROUPS = CHANNELS // (2 * P)
 
@@ -50,7 +48,7 @@ FLOPS = 2 * PIXELS * HIDDEN * (8 * CHANNELS) + 2 * PIXELS * HIDDEN * CHANNELS
 
 def tile_localpredictor_pa_k_kernel(tc, z, W1, b1, W2, b2, out):
     nc = tc.nc
-    z_view = z.rearrange("b (g a s e r j) h w -> g s e r a b (j h w)", g=GROUPS, a=A, s=2, e=2, r=2, j=2)
+    z_view = z.rearrange("b (t n j) h w -> t n b (j h w)", t=TILES, j=2)
     w1_view = W1.rearrange("(u p e) k -> u e p k", u=2, p=P, e=2)
     w2_view = W2.rearrange("(g p e) d -> p g (e d)", g=K_GROUPS, p=P, e=2)
     out_view = out.rearrange("b (g p e) h w -> g p b (e h w)", g=K_GROUPS, p=P, e=2)
@@ -68,36 +66,41 @@ def tile_localpredictor_pa_k_kernel(tc, z, W1, b1, W2, b2, out):
         sum_pool = ctx.enter_context(tc.psum_pool(name="sums", bufs=D_TILES))
         ctx.enter_context(tc.manual_schedule())
 
+        ident = keep.tile([P, P], F32)
+        make_identity(nc, ident[:])
+        permutation = keep.tile([P, P], BF16)
+        nc.gpsimd.tensor_copy(
+            out=permutation[:].rearrange("k (q a r) -> k q a r", q=4, r=2),
+            in_=ident[:].rearrange("k (a q r) -> k q a r", q=4, r=2),
+        )
+
         first_use = keep.tile([P, 1], F32)
         nc.vector.memset(first_use[:], 0.0)
         nc.scalar.activation(out=first_use[:], in_=first_use[:], func=ACT.Relu, scale=1.0)
 
         def load_maps(tile_index):
-            group, half = divmod(tile_index, 2)
             maps = z_pool.tile([P, BATCH, 2, SIDE, SIDE], BF16, tag="maps")
-            for e in range(2):
-                for r in range(2):
-                    nc.sync.dma_start(
-                        out=maps[64 * e + r : 64 * (e + 1) : 2].rearrange("p b j h w -> p b (j h w)"),
-                        in_=z_view[group, half, e, r],
-                    )
+            nc.sync.dma_start(out=maps[:].rearrange("p b j h w -> p b (j h w)"), in_=z_view[tile_index])
             return maps
 
-        def load_chunk(chunk):
-            group, d_tile = divmod(chunk, D_TILES)
+        def load_raw(step):
+            tile_index, d_tile = divmod(step, D_TILES)
             u, e = divmod(d_tile, 2)
-            raw = raw_pool.tile([P, GROUP_COLUMNS], BF16, tag="raw")
-            nc.sync.dma_start(out=raw[:], in_=w1_view[u, e, :, GROUP_COLUMNS * group : GROUP_COLUMNS * (group + 1)])
+            raw = raw_pool.tile([P, TILE_COLUMNS], BF16, tag="raw")
+            nc.sync.dma_start(out=raw[:], in_=w1_view[u, e, :, TILE_COLUMNS * tile_index : TILE_COLUMNS * (tile_index + 1)])
             return raw
 
-        maps = [load_maps(0), load_maps(1)]
+        maps = [load_maps(0)]
+        raws = [load_raw(0)]
+        maps.append(load_maps(1))
+        raws.append(load_raw(1))
         bias_rows = keep.tile([P, 2 * P], BF16)
-        nc.gpsimd.memset(bias_rows[:].bitcast(I32), 0)
+        nc.vector.memset(bias_rows[:].bitcast(I32), 0)
         nc.sync.dma_start(out=bias_rows[0:2, :], in_=b1.rearrange("(u x) -> u x", u=2))
         nc.sync.dma_start(out=bias_rows[2 : 2 + K_GROUPS, :], in_=b2.rearrange("(g x) -> g x", g=K_GROUPS))
-        raws = [load_chunk(0), load_chunk(1)]
-        maps.append(load_maps(2))
-        raws.extend([load_chunk(chunk) for chunk in range(2, RAW_AHEAD)])
+        raws.append(load_raw(2))
+        maps.extend([load_maps(2), load_maps(3)])
+        raws.extend([load_raw(step) for step in range(3, RAW_AHEAD)])
         w2_raw = keep.tile([P, K_GROUPS, 2, HIDDEN], BF16)
 
         pairs_tiles = [keep.tile([P, SIDE + 2, PITCH, BATCH], F32, name="pairs%d" % i) for i in range(2)]
@@ -111,15 +114,29 @@ def tile_localpredictor_pa_k_kernel(tc, z, W1, b1, W2, b2, out):
             for row in (0, SIDE + 1):
                 zero(side_tiles[i][:, row], 0.0)
 
-        ident = keep.tile([P, P], F32)
-        make_identity(nc, ident[:])
+        permuted_tiles = {}
 
-        def make_pairs(tile_index, engine_copy):
-            engine_copy(
+        def permute(tile_index):
+            permuted = turn_pool.tile([P, 4, P], F32, tag="turned", name="permuted")
+            words = permuted[:].rearrange("p k d -> p (k d)").bitcast(BF16).rearrange("p (x b j) -> p x b j", b=BATCH, j=2)
+            for b in range(BATCH):
+                nc.tensor.matmul(
+                    out=words[:, :, b, :],
+                    lhsT=permutation[:],
+                    rhs=maps[tile_index][:, b].rearrange("p j h w -> p (h w) j"),
+                    start=True,
+                    stop=True,
+                )
+            permuted_tiles[tile_index] = permuted
+
+        def make_pairs(tile_index):
+            nc.scalar.copy(
                 out=pairs_tiles[tile_index % 2][:, 1 : SIDE + 1, FIRST : FIRST + SIDE, :]
+                .bitcast(BF16),
+                in_=permuted_tiles[tile_index][:]
+                .rearrange("p k d -> p (k d)")
                 .bitcast(BF16)
-                .rearrange("p h w (b j) -> p h w b j", b=BATCH),
-                in_=maps[tile_index][:].rearrange("p b j h w -> p h w b j"),
+                .rearrange("p (h w x) -> p h w x", h=SIDE, w=SIDE),
             )
 
         def make_side(tile_index, part, engine_copy):
@@ -159,25 +176,18 @@ def tile_localpredictor_pa_k_kernel(tc, z, W1, b1, W2, b2, out):
                 in_=source.rearrange("p r c b u -> p (r c b u)").bitcast(BF16),
             )
 
-        steps = [(tile_index, d_tile) for d_tile in range(D_TILES) for tile_index in range(2)]
-        steps.extend([(tile_index, d_tile) for tile_index in range(2, TILES) for d_tile in range(D_TILES)])
         ordered_tiles = {}
 
-        def chunk_of(step):
-            tile_index, d_tile = steps[step]
-            return D_TILES * (tile_index // 2) + d_tile
-
         def sort_step(step):
-            half = steps[step][0] % 2
-            by_channel = raws[chunk_of(step)][:].rearrange("d (a s e c k) -> d s e a c k", a=A, s=2, e=2, c=4, k=WINDOW)
+            by_channel = raws[step][:].rearrange("d (a q c k) -> d q a c k", a=A, q=4, c=4, k=WINDOW)
             ordered = sorted_pool.tile([P, NEIGHBOURS, 2 * P], BF16, tag="ordered")
             for side_of_centre in range(2):
                 first = 4 * side_of_centre
                 on_scalar = side_of_centre == 1 and step in SCALAR_SORTS
                 engine_copy = nc.scalar.copy if on_scalar else nc.vector.tensor_copy
                 engine_copy(
-                    out=ordered[:, first : first + 4, :].rearrange("d k (e a c) -> d e a c k", e=2, c=4),
-                    in_=by_channel[:, half, :, :, :, first + side_of_centre : first + side_of_centre + 4],
+                    out=ordered[:, first : first + 4, :].rearrange("d k (q a c) -> d q a c k", q=4, c=4),
+                    in_=by_channel[:, :, :, :, first + side_of_centre : first + side_of_centre + 4],
                 )
             ordered_tiles[step] = ordered
 
@@ -190,6 +200,8 @@ def tile_localpredictor_pa_k_kernel(tc, z, W1, b1, W2, b2, out):
             items.append(("W1", step))
             if step in W2_AFTER:
                 items.append(("W2", W2_AFTER.index(step)))
+            if step in PERMUTE_AFTER:
+                items.append(("maps", PERMUTE_AFTER.index(step) + 1))
         place_of_step = [items.index(("W1", step)) for step in range(STEPS)]
 
         def planes_of(item):
@@ -208,6 +220,10 @@ def tile_localpredictor_pa_k_kernel(tc, z, W1, b1, W2, b2, out):
         codes_of = {}
 
         def turn(item):
+            if item[0] == "maps":
+                for half in range(2):
+                    permute(2 * item[1] + half)
+                return
             planes = planes_of(item)
             turned_tiles[item] = []
             for bank in range(2):
@@ -217,6 +233,10 @@ def tile_localpredictor_pa_k_kernel(tc, z, W1, b1, W2, b2, out):
                 turned_tiles[item].append(turned)
 
         def drain(item):
+            if item[0] == "maps":
+                for half in range(2):
+                    make_pairs(2 * item[1] + half)
+                return
             grouped = grouped_pool.tile([P, 2, 2, P, PACK], BF16, align_bytes=64, tag="grouped")
             for bank in range(2):
                 nc.scalar.copy(
@@ -227,6 +247,8 @@ def tile_localpredictor_pa_k_kernel(tc, z, W1, b1, W2, b2, out):
 
         def quantise(item):
             kind, index = item
+            if kind == "maps":
+                return
             if kind == "W1":
                 codes = w1q_pool.tile([P, WORDS * P], U32, align_bytes=64, tag="w1_codes")
                 scales = w1q_pool.tile([P, WORDS * P], U8, align_bytes=64, tag="w1_scales")
@@ -255,7 +277,7 @@ def tile_localpredictor_pa_k_kernel(tc, z, W1, b1, W2, b2, out):
                 )
 
         def multiply(step):
-            tile_index, d_tile = steps[step]
+            tile_index, d_tile = divmod(step, D_TILES)
             codes, scales = codes_of[("W1", step)]
             win_codes, win_scales = win_of[tile_index]
             for word in range(WORDS):
@@ -287,44 +309,34 @@ def tile_localpredictor_pa_k_kernel(tc, z, W1, b1, W2, b2, out):
 
         FIRST_TICK = -SORT_LEAD - 1
 
-        def window_jobs(tile_index):
-            copy = nc.vector.tensor_copy if tile_index == 0 else nc.scalar.copy
-            make = [
-                lambda: make_pairs(tile_index, copy),
-                lambda: (make_side(tile_index, 0, copy), make_side(tile_index, 1, copy)),
-                lambda: (make_updown(tile_index, 0, copy), make_updown(tile_index, 1, copy)),
-            ]
-            words = [lambda word=word: quantise_windows(tile_index, word) for word in range(WORDS)]
-            return make, words
-
-        make, words = window_jobs(0)
-        for job in [make[0], make[1], words[0], make[2], words[1], words[2], words[3]]:
-            at(FIRST_TICK, job)
-        at(FIRST_TICK, make_bias)
-        for tile_index in range(1, TILES):
-            first_step = min(step for step in range(STEPS) if steps[step][0] == tile_index)
-            start = max(tick_of(first_step - WINDOW_LEAD), FIRST_TICK)
-            make, words = window_jobs(tile_index)
-            for offset, job in [(0, make[0]), (1, make[1]), (2, make[2])]:
-                at(start + offset, job)
-            for word in range(WORDS):
-                at(start + 2 + word, words[word])
+        at(-1, make_bias)
 
         def sort_job(step):
             def work():
                 sort_step(step)
-                chunk = chunk_of(step) + RAW_AHEAD
-                if steps[step][0] % 2 == 1 and chunk < CHUNKS:
-                    raws.append(load_chunk(chunk))
+                if step + RAW_AHEAD < STEPS:
+                    raws.append(load_raw(step + RAW_AHEAD))
                 if step == W2_LOAD:
                     nc.sync.dma_start(out=w2_raw[:].rearrange("p g e d -> p g (e d)"), in_=w2_view)
-                if step % D_TILES == MAPS_LOAD and len(maps) < TILES:
+                if step % 2 == 0 and len(maps) < TILES:
                     maps.append(load_maps(len(maps)))
 
             return work
 
         for step in range(STEPS):
             at(tick_of(step - SORT_LEAD), sort_job(step))
+        at(FIRST_TICK, lambda: (permute(0), permute(1), make_pairs(0)))
+        for tile_index in range(TILES):
+            start = max(tick_of(D_TILES * tile_index - WINDOW_LEAD), FIRST_TICK)
+            updown = start if tile_index == 0 else start + 2
+            for part in range(2):
+                at(start, lambda t=tile_index, part=part: make_side(t, part, nc.scalar.copy))
+            for part in range(2):
+                at(updown, lambda t=tile_index, part=part: make_updown(t, part, nc.scalar.copy))
+            for word in range(WORDS):
+                at(start + 1 + word, lambda t=tile_index, word=word: quantise_windows(t, word))
+            if tile_index == 0:
+                at(start, lambda: make_pairs(1))
 
         for n in range(FIRST_TICK, len(items) + 3):
             if 0 <= n + 1 < len(items):
@@ -336,7 +348,7 @@ def tile_localpredictor_pa_k_kernel(tc, z, W1, b1, W2, b2, out):
             if 0 <= n - 2 < len(items) and items[n - 2][0] == "W1":
                 multiply(items[n - 2][1])
             if 0 <= n - 3 < len(items) and items[n - 3][1] >= STEPS - D_TILES:
-                relu(steps[items[n - 3][1]][1])
+                relu(items[n - 3][1] % D_TILES)
             for job in jobs.get(n, []):
                 job()
 

@@ -32,7 +32,6 @@ FIRST = 2
 
 D_TILES = HIDDEN // P
 STEPS = TILES * D_TILES
-W2_CALLS = 4
 W2_AFTER = [14, 18, 22, 26]
 RAW_AHEAD = 10
 W2_LOAD = 7
@@ -41,7 +40,8 @@ SCALAR_SORTS = list(range(6, 31, 3))
 SORT_LEAD = 3
 WINDOW_LEAD = 5
 
-K_GROUPS = CHANNELS // (2 * P)
+K_RUN = 4
+K_GROUPS = CHANNELS // (K_RUN * P)
 
 FLOPS = 2 * PIXELS * HIDDEN * (8 * CHANNELS) + 2 * PIXELS * HIDDEN * CHANNELS
 
@@ -50,18 +50,18 @@ def tile_localpredictor_pa_k_kernel(tc, z, W1, b1, W2, b2, out):
     nc = tc.nc
     z_view = z.rearrange("b (t n j) h w -> t n b (j h w)", t=TILES, j=2)
     w1_view = W1.rearrange("(u p e) k -> u e p k", u=2, p=P, e=2)
-    w2_view = W2.rearrange("(g p e) d -> p g (e d)", g=K_GROUPS, p=P, e=2)
-    out_view = out.rearrange("b (g p e) h w -> g p b (e h w)", g=K_GROUPS, p=P, e=2)
+    w2_view = W2.rearrange("(g p e) d -> p g (e d)", g=K_GROUPS, p=P, e=K_RUN)
+    out_view = out.rearrange("b (g p e) h w -> g p b (e h w)", g=K_GROUPS, p=P, e=K_RUN)
 
     with ExitStack() as ctx:
         keep = ctx.enter_context(tc.tile_pool(name="keep", bufs=1))
-        z_pool = ctx.enter_context(tc.tile_pool(name="z", bufs=TILES))
+        z_pool = ctx.enter_context(tc.tile_pool(name="z", bufs=6))
         raw_pool = ctx.enter_context(tc.tile_pool(name="raw", bufs=RAW_AHEAD))
         win_pool = ctx.enter_context(tc.tile_pool(name="win", bufs=4))
         sorted_pool = ctx.enter_context(tc.tile_pool(name="sorted", bufs=SORT_LEAD + 2))
         grouped_pool = ctx.enter_context(tc.tile_pool(name="grouped", bufs=3))
         w1q_pool = ctx.enter_context(tc.tile_pool(name="w1q", bufs=3))
-        res_pool = ctx.enter_context(tc.tile_pool(name="res", bufs=6))
+        res_pool = ctx.enter_context(tc.tile_pool(name="res", bufs=2 * K_GROUPS))
         turn_pool = ctx.enter_context(tc.psum_pool(name="turn", bufs=4))
         sum_pool = ctx.enter_context(tc.psum_pool(name="sums", bufs=D_TILES))
         ctx.enter_context(tc.manual_schedule())
@@ -94,14 +94,14 @@ def tile_localpredictor_pa_k_kernel(tc, z, W1, b1, W2, b2, out):
         raws = [load_raw(0)]
         maps.append(load_maps(1))
         raws.append(load_raw(1))
-        bias_rows = keep.tile([P, 2 * P], BF16)
+        bias_rows = keep.tile([P, K_RUN * P], BF16)
         nc.vector.memset(bias_rows[:].bitcast(I32), 0)
-        nc.sync.dma_start(out=bias_rows[0:2, :], in_=b1.rearrange("(u x) -> u x", u=2))
+        nc.sync.dma_start(out=bias_rows[0:2, 0 : 2 * P], in_=b1.rearrange("(u x) -> u x", u=2))
         nc.sync.dma_start(out=bias_rows[2 : 2 + K_GROUPS, :], in_=b2.rearrange("(g x) -> g x", g=K_GROUPS))
         raws.append(load_raw(2))
         maps.extend([load_maps(2), load_maps(3)])
         raws.extend([load_raw(step) for step in range(3, RAW_AHEAD)])
-        w2_raw = keep.tile([P, K_GROUPS, 2, HIDDEN], BF16)
+        w2_raw = keep.tile([P, K_GROUPS, K_RUN, HIDDEN], BF16)
 
         pairs_tiles = [keep.tile([P, SIDE + 2, PITCH, BATCH], F32, name="pairs%d" % i) for i in range(2)]
         side_tiles = [
@@ -191,8 +191,8 @@ def tile_localpredictor_pa_k_kernel(tc, z, W1, b1, W2, b2, out):
                 )
             ordered_tiles[step] = ordered
 
-        w2_codes = keep.tile([P, 2 * K_GROUPS * P], U32, align_bytes=64)
-        w2_scales = keep.tile([P, 2 * K_GROUPS * P], U8, align_bytes=64)
+        w2_codes = keep.tile([P, CHANNELS], U32, align_bytes=64)
+        w2_scales = keep.tile([P, CHANNELS], U8, align_bytes=64)
         neighbour_of = [position - (position > WINDOW // 2) for pair in WORD_POSITIONS for position in pair]
 
         items = []
@@ -209,10 +209,7 @@ def tile_localpredictor_pa_k_kernel(tc, z, W1, b1, W2, b2, out):
             if kind == "W1":
                 return [ordered_tiles[index][:, n, :].bitcast(F32) for n in neighbour_of]
             return [
-                w2_raw[:, 2 * index + g, e, 2 * P * u : 2 * P * (u + 1)].bitcast(F32)
-                for g in range(2)
-                for e in range(2)
-                for u in range(2)
+                w2_raw[:, index, e, 2 * P * u : 2 * P * (u + 1)].bitcast(F32) for e in range(K_RUN) for u in range(2)
             ]
 
         turned_tiles = {}
@@ -272,7 +269,7 @@ def tile_localpredictor_pa_k_kernel(tc, z, W1, b1, W2, b2, out):
                     out=hidden[:, d_tile, image, :],
                     in_=sums[d_tile][:].rearrange("p (x b) -> p b x", b=BATCH)[:, image],
                     func=ACT.Relu,
-                    bias=bias[:, d_tile : d_tile + 1],
+                    bias=bias1[:, d_tile : d_tile + 1],
                     scale=1.0,
                 )
 
@@ -292,12 +289,20 @@ def tile_localpredictor_pa_k_kernel(tc, z, W1, b1, W2, b2, out):
                     stop=(tile_index == TILES - 1 and word == WORDS - 1),
                 )
 
-        bias = keep.tile([P, 2 * (2 + K_GROUPS)], F32)
+        bias1 = keep.tile([P, D_TILES], F32)
+        bias2 = keep.tile([P, K_GROUPS, K_RUN], F32)
 
         def make_bias():
-            bias_turned = turn_pool.tile([P, 4, P], F32, tag="turned")
-            nc.tensor.transpose(bias_turned[:, 0, :], bias_rows[:].bitcast(F32), ident[:])
-            nc.vector.tensor_copy(out=bias[:], in_=bias_turned[:, 0, 0 : 2 + K_GROUPS].bitcast(BF16))
+            turned = turn_pool.tile([P, 4, P], F32, tag="turned")
+            words = bias_rows[:].bitcast(F32)
+            nc.tensor.transpose(turned[:, 0, :], words[:, 0:P], ident[:])
+            for half in range(2):
+                nc.tensor.transpose(turned[:, 1 + half, :], words[:, half : 2 * P : 2], ident[:])
+            nc.vector.tensor_copy(out=bias1[:], in_=turned[:, 0, 0:2].bitcast(BF16))
+            nc.vector.tensor_copy(
+                out=bias2[:].rearrange("p g (h j) -> p g h j", h=2),
+                in_=turned[:, 1:3, 2 : 2 + K_GROUPS].bitcast(BF16).rearrange("p h (g j) -> p g h j", j=2),
+            )
 
         jobs = {}
 
@@ -366,23 +371,26 @@ def tile_localpredictor_pa_k_kernel(tc, z, W1, b1, W2, b2, out):
             )
         for b in range(BATCH):
             for g in range(K_GROUPS):
-                logits = sum_pool.tile([P, 2, IMAGE], F32, tag="sums")
-                res = res_pool.tile([P, 2, IMAGE], F32, tag="res")
-                for e in range(2):
-                    rows = slice(P * (2 * g + e), P * (2 * g + e + 1))
-                    nc.tensor.matmul_mx(
-                        out=logits[:, e],
-                        lhsT=w2_codes[:, rows].bitcast(FP8X4),
-                        lhsT_scale=w2_scales[:, rows],
-                        rhs=hidden_codes[:, b].bitcast(FP8X4),
-                        rhs_scale=hidden_scales[:, b],
-                        start=True,
-                        stop=True,
-                    )
-                for e in range(2):
-                    b2_column = bias[:, 4 + 2 * g + e : 5 + 2 * g + e]
-                    if g % 2 == 0:
-                        nc.scalar.activation(out=res[:, e], in_=logits[:, e], func=ACT.Identity, bias=b2_column, scale=1.0)
-                    else:
-                        nc.vector.tensor_scalar_add(out=res[:, e], in0=logits[:, e], scalar1=b2_column)
+                res = res_pool.tile([P, K_RUN, IMAGE], F32, tag="res")
+                for half in range(2):
+                    logits = sum_pool.tile([P, 2, IMAGE], F32, tag="sums", name="logits")
+                    for j in range(2):
+                        e = 2 * half + j
+                        rows = slice(P * (K_RUN * g + e), P * (K_RUN * g + e + 1))
+                        nc.tensor.matmul_mx(
+                            out=logits[:, j],
+                            lhsT=w2_codes[:, rows].bitcast(FP8X4),
+                            lhsT_scale=w2_scales[:, rows],
+                            rhs=hidden_codes[:, b].bitcast(FP8X4),
+                            rhs_scale=hidden_scales[:, b],
+                            start=True,
+                            stop=True,
+                        )
+                    for j in range(2):
+                        e = 2 * half + j
+                        b2_column = bias2[:, g, e : e + 1]
+                        if half == 0:
+                            nc.scalar.activation(out=res[:, e], in_=logits[:, j], func=ACT.Identity, bias=b2_column, scale=1.0)
+                        else:
+                            nc.vector.tensor_scalar_add(out=res[:, e], in0=logits[:, j], scalar1=b2_column)
                 nc.sync.dma_start(out=out_view[g, :, b], in_=res[:].rearrange("p e x -> p (e x)"))

@@ -55,12 +55,12 @@ def tile_localpredictor_pa_k_kernel(tc, z, W1, b1, W2, b2, out):
 
     with ExitStack() as ctx:
         keep = ctx.enter_context(tc.tile_pool(name="keep", bufs=1))
-        z_pool = ctx.enter_context(tc.tile_pool(name="z", bufs=6))
+        z_pool = ctx.enter_context(tc.tile_pool(name="z", bufs=5))
         raw_pool = ctx.enter_context(tc.tile_pool(name="raw", bufs=RAW_AHEAD))
         win_pool = ctx.enter_context(tc.tile_pool(name="win", bufs=4))
         sorted_pool = ctx.enter_context(tc.tile_pool(name="sorted", bufs=SORT_LEAD + 2))
-        grouped_pool = ctx.enter_context(tc.tile_pool(name="grouped", bufs=3))
-        w1q_pool = ctx.enter_context(tc.tile_pool(name="w1q", bufs=3))
+        grouped_pool = ctx.enter_context(tc.tile_pool(name="grouped", bufs=4))
+        w1q_pool = ctx.enter_context(tc.tile_pool(name="w1q", bufs=4))
         res_pool = ctx.enter_context(tc.tile_pool(name="res", bufs=2 * K_GROUPS))
         turn_pool = ctx.enter_context(tc.psum_pool(name="turn", bufs=4))
         sum_pool = ctx.enter_context(tc.psum_pool(name="sums", bufs=D_TILES))

@@ -10,6 +10,7 @@ U32 = mybir.dt.uint32
 U8 = mybir.dt.uint8
 FP8X4 = mybir.dt.float8_e4m3fn_x4
 ACT = mybir.ActivationFunctionType
+ALU = mybir.AluOpType
 
 P = 128
 PACK = 4
@@ -265,13 +266,13 @@ def tile_localpredictor_pa_k_kernel(tc, z, W1, b1, W2, b2, out):
         def relu(d_tile):
             images = [slice(0, BATCH)] if d_tile < D_TILES - 1 else [slice(b, b + 1) for b in range(BATCH)]
             for image in images:
-                nc.scalar.activation(
-                    out=hidden[:, d_tile, image, :],
-                    in_=sums[d_tile][:].rearrange("p (x b) -> p b x", b=BATCH)[:, image],
-                    func=ACT.Relu,
-                    bias=bias1[:, d_tile : d_tile + 1],
-                    scale=1.0,
-                )
+                result = hidden[:, d_tile, image, :]
+                values = sums[d_tile][:].rearrange("p (x b) -> p b x", b=BATCH)[:, image]
+                bias = bias1[:, d_tile : d_tile + 1]
+                if len(images) == BATCH and image.start == 0:
+                    nc.vector.tensor_scalar(out=result, in0=values, scalar1=bias, scalar2=0.0, op0=ALU.add, op1=ALU.max)
+                else:
+                    nc.scalar.activation(out=result, in_=values, func=ACT.Relu, bias=bias, scale=1.0)
 
         def multiply(step):
             tile_index, d_tile = divmod(step, D_TILES)
@@ -372,25 +373,30 @@ def tile_localpredictor_pa_k_kernel(tc, z, W1, b1, W2, b2, out):
         for b in range(BATCH):
             for g in range(K_GROUPS):
                 res = res_pool.tile([P, K_RUN, IMAGE], F32, tag="res")
-                for half in range(2):
-                    logits = sum_pool.tile([P, 2, IMAGE], F32, tag="sums", name="logits")
-                    for j in range(2):
-                        e = 2 * half + j
-                        rows = slice(P * (K_RUN * g + e), P * (K_RUN * g + e + 1))
-                        nc.tensor.matmul_mx(
-                            out=logits[:, j],
-                            lhsT=w2_codes[:, rows].bitcast(FP8X4),
-                            lhsT_scale=w2_scales[:, rows],
-                            rhs=hidden_codes[:, b].bitcast(FP8X4),
-                            rhs_scale=hidden_scales[:, b],
-                            start=True,
-                            stop=True,
+                pieces = 2 if b == 0 and g == 0 else 1
+                for e in range(K_RUN):
+                    if (K_RUN * g + e) % 4 < 2:
+                        logits = sum_pool.tile([P, IMAGE], F32, tag="sums", name="logits")
+                    else:
+                        logits = turn_pool.tile([P, IMAGE], F32, tag="turned", name="logits")
+                    rows = slice(P * (K_RUN * g + e), P * (K_RUN * g + e + 1))
+                    nc.tensor.matmul_mx(
+                        out=logits[:],
+                        lhsT=w2_codes[:, rows].bitcast(FP8X4),
+                        lhsT_scale=w2_scales[:, rows],
+                        rhs=hidden_codes[:, b].bitcast(FP8X4),
+                        rhs_scale=hidden_scales[:, b],
+                        start=True,
+                        stop=True,
+                    )
+                    b2_column = bias2[:, g, e : e + 1]
+                    if e % 2 == 0:
+                        nc.scalar.activation(out=res[:, e], in_=logits[:], func=ACT.Identity, bias=b2_column, scale=1.0)
+                    else:
+                        nc.vector.tensor_scalar_add(out=res[:, e], in0=logits[:], scalar1=b2_column)
+                    if (e + 1) % (K_RUN // pieces) == 0:
+                        ready = slice(e + 1 - K_RUN // pieces, e + 1)
+                        nc.sync.dma_start(
+                            out=out_view[g, :, b, IMAGE * ready.start : IMAGE * ready.stop],
+                            in_=res[:, ready].rearrange("p e x -> p (e x)"),
                         )
-                    for j in range(2):
-                        e = 2 * half + j
-                        b2_column = bias2[:, g, e : e + 1]
-                        if half == 0:
-                            nc.scalar.activation(out=res[:, e], in_=logits[:, j], func=ACT.Identity, bias=b2_column, scale=1.0)
-                        else:
-                            nc.vector.tensor_scalar_add(out=res[:, e], in0=logits[:, j], scalar1=b2_column)
-                nc.sync.dma_start(out=out_view[g, :, b], in_=res[:].rearrange("p e x -> p (e x)"))

from contextlib import ExitStack

import concourse.mybir as mybir
from concourse.masks import make_identity

BF16 = mybir.dt.bfloat16
F32 = mybir.dt.float32
I32 = mybir.dt.int32
U32 = mybir.dt.uint32
U8 = mybir.dt.uint8
FP8X4 = mybir.dt.float8_e4m3fn_x4
ACT = mybir.ActivationFunctionType
ALU = mybir.AluOpType

P = 128
PACK = 4
BATCH, CHANNELS, SIDE, HIDDEN = 2, 2048, 16, 512
WINDOW = 9
IMAGE = SIDE * SIDE
PIXELS = BATCH * IMAGE

TILES = 8
TILE_CHANNELS = CHANNELS // TILES
A = TILE_CHANNELS // 16
TILE_COLUMNS = TILE_CHANNELS * WINDOW

WORDS = 4
WORD_POSITIONS = [[3 * di, 3 * di + 2] for di in range(3)] + [[1, 7]]
NEIGHBOURS = 2 * WORDS

PITCH = 20
FIRST = 2

D_TILES = HIDDEN // P
STEPS = TILES * D_TILES
W2_AFTER = [14, 18, 22, 26]
RAW_AHEAD = 10
W2_LOAD = 7
PERMUTE_AFTER = [1, 9, 17]
SCALAR_SORTS = list(range(6, 31, 3))
SORT_LEAD = 3
WINDOW_LEAD = 5

K_RUN = 4
K_GROUPS = CHANNELS // (K_RUN * P)

FLOPS = 2 * PIXELS * HIDDEN * (8 * CHANNELS) + 2 * PIXELS * HIDDEN * CHANNELS


def tile_localpredictor_pa_k_kernel(tc, z, W1, b1, W2, b2, out):
    nc = tc.nc
    z_view = z.rearrange("b (t n j) h w -> t n b (j h w)", t=TILES, j=2)
    w1_view = W1.rearrange("(u p e) k -> u e p k", u=2, p=P, e=2)
    w2_view = W2.rearrange("(g p e) d -> p g (e d)", g=K_GROUPS, p=P, e=K_RUN)
    out_view = out.rearrange("b (g p e) h w -> g p b (e h w)", g=K_GROUPS, p=P, e=K_RUN)

    with ExitStack() as ctx:
        keep = ctx.enter_context(tc.tile_pool(name="keep", bufs=1))
        z_pool = ctx.enter_context(tc.tile_pool(name="z", bufs=5))
        raw_pool = ctx.enter_context(tc.tile_pool(name="raw", bufs=RAW_AHEAD))
        win_pool = ctx.enter_context(tc.tile_pool(name="win", bufs=4))
        sorted_pool = ctx.enter_context(tc.tile_pool(name="sorted", bufs=SORT_LEAD + 2))
        grouped_pool = ctx.enter_context(tc.tile_pool(name="grouped", bufs=4))
        w1q_pool = ctx.enter_context(tc.tile_pool(name="w1q", bufs=4))
        res_pool = ctx.enter_context(tc.tile_pool(name="res", bufs=2 * K_GROUPS))
        turn_pool = ctx.enter_context(tc.psum_pool(name="turn", bufs=4))
        sum_pool = ctx.enter_context(tc.psum_pool(name="sums", bufs=D_TILES))
        ctx.enter_context(tc.manual_schedule())

        ident = keep.tile([P, P], F32)
        make_identity(nc, ident[:])
        permutation = keep.tile([P, P], BF16)
        nc.gpsimd.tensor_copy(
            out=permutation[:].rearrange("k (q a r) -> k q a r", q=4, r=2),
            in_=ident[:].rearrange("k (a q r) -> k q a r", q=4, r=2),
        )

        first_use = keep.tile([P, 1], F32)
        nc.vector.memset(first_use[:], 0.0)
        nc.scalar.activation(out=first_use[:], in_=first_use[:], func=ACT.Relu, scale=1.0)

        def load_maps(tile_index):
            maps = z_pool.tile([P, BATCH, 2, SIDE, SIDE], BF16, tag="maps")
            nc.sync.dma_start(out=maps[:].rearrange("p b j h w -> p b (j h w)"), in_=z_view[tile_index])
            return maps

        def load_raw(step):
            tile_index, d_tile = divmod(step, D_TILES)
            u, e = divmod(d_tile, 2)
            raw = raw_pool.tile([P, TILE_COLUMNS], BF16, tag="raw")
            nc.sync.dma_start(out=raw[:], in_=w1_view[u, e, :, TILE_COLUMNS * tile_index : TILE_COLUMNS * (tile_index + 1)])
            return raw

        maps = [load_maps(0)]
        raws = [load_raw(0)]
        maps.append(load_maps(1))
        raws.append(load_raw(1))
        bias_rows = keep.tile([P, K_RUN * P], BF16)
        nc.vector.memset(bias_rows[:].bitcast(I32), 0)
        nc.sync.dma_start(out=bias_rows[0:2, 0 : 2 * P], in_=b1.rearrange("(u x) -> u x", u=2))
        nc.sync.dma_start(out=bias_rows[2 : 2 + K_GROUPS, :], in_=b2.rearrange("(g x) -> g x", g=K_GROUPS))
        raws.append(load_raw(2))
        maps.extend([load_maps(2), load_maps(3)])
        raws.extend([load_raw(step) for step in range(3, RAW_AHEAD)])
        w2_raw = keep.tile([P, K_GROUPS, K_RUN, HIDDEN], BF16)

        pairs_tiles = [keep.tile([P, SIDE + 2, PITCH, BATCH], F32, name="pairs%d" % i) for i in range(2)]
        side_tiles = [
            keep.tile([P, SIDE + 2, SIDE, BATCH, 2], F32, align_bytes=64, name="side%d" % i) for i in range(2)
        ]
        updown_tiles = [keep.tile([P, SIDE, SIDE, BATCH, 2], F32, align_bytes=64, name="updown%d" % i) for i in range(2)]
        for i in range(2):
            zero = nc.vector.memset if i == 0 else nc.gpsimd.memset
            zero(pairs_tiles[i][:], 0.0)
            for row in (0, SIDE + 1):
                zero(side_tiles[i][:, row], 0.0)

        permuted_tiles = {}

        def permute(tile_index):
            permuted = turn_pool.tile([P, 4, P], F32, tag="turned", name="permuted")
            words = permuted[:].rearrange("p k d -> p (k d)").bitcast(BF16).rearrange("p (x b j) -> p x b j", b=BATCH, j=2)
            for b in range(BATCH):
                nc.tensor.matmul(
                    out=words[:, :, b, :],
                    lhsT=permutation[:],
                    rhs=maps[tile_index][:, b].rearrange("p j h w -> p (h w) j"),
                    start=True,
                    stop=True,
                )
            permuted_tiles[tile_index] = permuted

        def make_pairs(tile_index):
            nc.scalar.copy(
                out=pairs_tiles[tile_index % 2][:, 1 : SIDE + 1, FIRST : FIRST + SIDE, :]
                .bitcast(BF16),
                in_=permuted_tiles[tile_index][:]
                .rearrange("p k d -> p (k d)")
                .bitcast(BF16)
                .rearrange("p (h w x) -> p h w x", h=SIDE, w=SIDE),
            )

        def make_side(tile_index, part, engine_copy):
            first = FIRST - 1 + 2 * part
            engine_copy(
                out=side_tiles[tile_index % 2][:, 1 : SIDE + 1].rearrange(
                    "p r (q h m) b u -> p h r q m b u", h=2, m=2
                )[:, part],
                in_=pairs_tiles[tile_index % 2][:, 1 : SIDE + 1, first : first + SIDE, :].rearrange(
                    "p r (q u m) b -> p r q m b u", u=2, m=2
                ),
            )

        def make_updown(tile_index, part, engine_copy):
            engine_copy(
                out=updown_tiles[tile_index % 2][:].rearrange("p (q h m) c b u -> p h q m c b u", h=2, m=2)[:, part],
                in_=pairs_tiles[tile_index % 2][:, 2 * part : 2 * part + SIDE, FIRST : FIRST + SIDE, :].rearrange(
                    "p (q u m) c b -> p q m c b u", u=2, m=2
                ),
            )

        win_of = {}

        def quantise_windows(tile_index, word):
            if tile_index not in win_of:
                codes = win_pool.tile([P, WORDS, PIXELS], U32, align_bytes=64, tag="win_codes", name="win_codes")
                scales = win_pool.tile([P, WORDS, PIXELS], U8, align_bytes=64, tag="win_scales", name="win_scales")
                win_of[tile_index] = (codes, scales)
            codes, scales = win_of[tile_index]
            if word < 3:
                source = side_tiles[tile_index % 2][:, word : word + SIDE]
            else:
                source = updown_tiles[tile_index % 2][:]
            nc.vector.quantize_mx(
                out=codes[:, word, :].bitcast(FP8X4),
                scales=scales[:, word, :],
                in_=source.rearrange("p r c b u -> p (r c b u)").bitcast(BF16),
            )

        ordered_tiles = {}

        def sort_step(step):
            by_channel = raws[step][:].rearrange("d (a q c k) -> d q a c k", a=A, q=4, c=4, k=WINDOW)
            ordered = sorted_pool.tile([P, NEIGHBOURS, 2 * P], BF16, tag="ordered")
            for side_of_centre in range(2):
                first = 4 * side_of_centre
                on_scalar = side_of_centre == 1 and step in SCALAR_SORTS
                engine_copy = nc.scalar.copy if on_scalar else nc.vector.tensor_copy
                engine_copy(
                    out=ordered[:, first : first + 4, :].rearrange("d k (q a c) -> d q a c k", q=4, c=4),
                    in_=by_channel[:, :, :, :, first + side_of_centre : first + side_of_centre + 4],
                )
            ordered_tiles[step] = ordered

        w2_codes = keep.tile([P, CHANNELS], U32, align_bytes=64)
        w2_scales = keep.tile([P, CHANNELS], U8, align_bytes=64)
        neighbour_of = [position - (position > WINDOW // 2) for pair in WORD_POSITIONS for position in pair]

        items = []
        for step in range(STEPS):
            items.append(("W1", step))
            if step in W2_AFTER:
                items.append(("W2", W2_AFTER.index(step)))
            if step in PERMUTE_AFTER:
                items.append(("maps", PERMUTE_AFTER.index(step) + 1))
        place_of_step = [items.index(("W1", step)) for step in range(STEPS)]

        def planes_of(item):
            kind, index = item
            if kind == "W1":
                return [ordered_tiles[index][:, n, :].bitcast(F32) for n in neighbour_of]
            return [
                w2_raw[:, index, e, 2 * P * u : 2 * P * (u + 1)].bitcast(F32) for e in range(K_RUN) for u in range(2)
            ]

        turned_tiles = {}
        grouped_tiles = {}
        codes_of = {}

        def turn(item):
            if item[0] == "maps":
                for half in range(2):
                    permute(2 * item[1] + half)
                return
            planes = planes_of(item)
            turned_tiles[item] = []
            for bank in range(2):
                turned = turn_pool.tile([P, 4, P], F32, tag="turned")
                for k in range(4):
                    nc.tensor.transpose(turned[:, k, :], planes[4 * bank + k], ident[:])
                turned_tiles[item].append(turned)

        def drain(item):
            if item[0] == "maps":
                for half in range(2):
                    make_pairs(2 * item[1] + half)
                return
            grouped = grouped_pool.tile([P, 2, 2, P, PACK], BF16, align_bytes=64, tag="grouped")
            for bank in range(2):
                nc.scalar.copy(
                    out=grouped[:, bank].bitcast(F32),
                    in_=turned_tiles[item][bank][:].rearrange("p (s u) d -> p s d u", u=2),
                )
            grouped_tiles[item] = grouped

        def quantise(item):
            kind, index = item
            if kind == "maps":
                return
            if kind == "W1":
                codes = w1q_pool.tile([P, WORDS * P], U32, align_bytes=64, tag="w1_codes")
                scales = w1q_pool.tile([P, WORDS * P], U8, align_bytes=64, tag="w1_scales")
                codes_of[item] = (codes[:], scales[:])
            else:
                columns = slice(WORDS * P * index, WORDS * P * (index + 1))
                codes_of[item] = (w2_codes[:, columns], w2_scales[:, columns])
            nc.vector.quantize_mx(
                out=codes_of[item][0].bitcast(FP8X4),
                scales=codes_of[item][1],
                in_=grouped_tiles[item][:].rearrange("p a s d t -> p (a s d t)"),
            )

        sums = [sum_pool.tile([P, PIXELS], F32, tag="sums", name="hidden_sums%d" % i) for i in range(D_TILES)]
        hidden = keep.tile([P, D_TILES, BATCH, IMAGE], BF16)

        def relu(d_tile):
            images = [slice(0, BATCH)] if d_tile < D_TILES - 1 else [slice(b, b + 1) for b in range(BATCH)]
            for image in images:
                result = hidden[:, d_tile, image, :]
                values = sums[d_tile][:].rearrange("p (x b) -> p b x", b=BATCH)[:, image]
                bias = bias1[:, d_tile : d_tile + 1]
                if len(images) == BATCH and image.start == 0:
                    nc.vector.tensor_scalar(out=result, in0=values, scalar1=bias, scalar2=0.0, op0=ALU.add, op1=ALU.max)
                else:
                    nc.scalar.activation(out=result, in_=values, func=ACT.Relu, bias=bias, scale=1.0)

        def multiply(step):
            tile_index, d_tile = divmod(step, D_TILES)
            codes, scales = codes_of[("W1", step)]
            win_codes, win_scales = win_of[tile_index]
            for word in range(WORDS):
                rows = slice(P * word, P * (word + 1))
                nc.tensor.matmul_mx(
                    out=sums[d_tile][:],
                    lhsT=codes[:, rows].bitcast(FP8X4),
                    lhsT_scale=scales[:, rows],
                    rhs=win_codes[:, word, :].bitcast(FP8X4),
                    rhs_scale=win_scales[:, word, :],
                    start=(tile_index == 0 and word == 0),
                    stop=(tile_index == TILES - 1 and word == WORDS - 1),
                )

        bias1 = keep.tile([P, D_TILES], F32)
        bias2 = keep.tile([P, K_GROUPS, K_RUN], F32)

        def make_bias():
            turned = turn_pool.tile([P, 4, P], F32, tag="turned")
            words = bias_rows[:].bitcast(F32)
            nc.tensor.transpose(turned[:, 0, :], words[:, 0:P], ident[:])
            for half in range(2):
                nc.tensor.transpose(turned[:, 1 + half, :], words[:, half : 2 * P : 2], ident[:])
            nc.vector.tensor_copy(out=bias1[:], in_=turned[:, 0, 0:2].bitcast(BF16))
            nc.vector.tensor_copy(
                out=bias2[:].rearrange("p g (h j) -> p g h j", h=2),
                in_=turned[:, 1:3, 2 : 2 + K_GROUPS].bitcast(BF16).rearrange("p h (g j) -> p g h j", j=2),
            )

        jobs = {}

        def at(tick, job):
            jobs.setdefault(tick, []).append(job)

        def tick_of(step):
            return place_of_step[step] if step >= 0 else step

        FIRST_TICK = -SORT_LEAD - 1

        at(-1, make_bias)

        def sort_job(step):
            def work():
                sort_step(step)
                if step + RAW_AHEAD < STEPS:
                    raws.append(load_raw(step + RAW_AHEAD))
                if step == W2_LOAD:
                    nc.sync.dma_start(out=w2_raw[:].rearrange("p g e d -> p g (e d)"), in_=w2_view)
                if step % 2 == 0 and len(maps) < TILES:
                    maps.append(load_maps(len(maps)))

            return work

        for step in range(STEPS):
            at(tick_of(step - SORT_LEAD), sort_job(step))
        at(FIRST_TICK, lambda: (permute(0), permute(1), make_pairs(0)))
        for tile_index in range(TILES):
            start = max(tick_of(D_TILES * tile_index - WINDOW_LEAD), FIRST_TICK)
            updown = start if tile_index == 0 else start + 2
            for part in range(2):
                at(start, lambda t=tile_index, part=part: make_side(t, part, nc.scalar.copy))
            for part in range(2):
                at(updown, lambda t=tile_index, part=part: make_updown(t, part, nc.scalar.copy))
            for word in range(WORDS):
                at(start + 1 + word, lambda t=tile_index, word=word: quantise_windows(t, word))
            if tile_index == 0:
                at(start, lambda: make_pairs(1))

        for n in range(FIRST_TICK, len(items) + 3):
            if 0 <= n + 1 < len(items):
                turn(items[n + 1])
            if 0 <= n < len(items):
                drain(items[n])
            if 0 <= n - 1 < len(items):
                quantise(items[n - 1])
            if 0 <= n - 2 < len(items) and items[n - 2][0] == "W1":
                multiply(items[n - 2][1])
            if 0 <= n - 3 < len(items) and items[n - 3][1] >= STEPS - D_TILES:
                relu(items[n - 3][1] % D_TILES)
            for job in jobs.get(n, []):
                job()

        hidden_codes = keep.tile([P, BATCH, IMAGE], U32, align_bytes=64)
        hidden_scales = keep.tile([P, BATCH, IMAGE], U8, align_bytes=64)
        hidden_grouped = keep.tile([P, BATCH, IMAGE, PACK], BF16, align_bytes=64)
        for b in range(BATCH):
            engine_copy = nc.vector.tensor_copy if b == 0 else nc.scalar.copy
            engine_copy(out=hidden_grouped[:, b], in_=hidden[:, :, b, :].rearrange("p t x -> p x t"))
        for b in range(BATCH):
            nc.vector.quantize_mx(
                out=hidden_codes[:, b].bitcast(FP8X4),
                scales=hidden_scales[:, b],
                in_=hidden_grouped[:, b].rearrange("p x t -> p (x t)"),
            )
        for b in range(BATCH):
            for g in range(K_GROUPS):
                res = res_pool.tile([P, K_RUN, IMAGE], F32, tag="res")
                pieces = 2 if b == 0 and g == 0 else 1
                for e in range(K_RUN):
                    if (K_RUN * g + e) % 4 < 2:
                        logits = sum_pool.tile([P, IMAGE], F32, tag="sums", name="logits")
                    else:
                        logits = turn_pool.tile([P, IMAGE], F32, tag="turned", name="logits")
                    rows = slice(P * (K_RUN * g + e), P * (K_RUN * g + e + 1))
                    nc.tensor.matmul_mx(
                        out=logits[:],
                        lhsT=w2_codes[:, rows].bitcast(FP8X4),
                        lhsT_scale=w2_scales[:, rows],
                        rhs=hidden_codes[:, b].bitcast(FP8X4),
                        rhs_scale=hidden_scales[:, b],
                        start=True,
                        stop=True,
                    )
                    b2_column = bias2[:, g, e : e + 1]
                    if e % 2 == 0:
                        nc.scalar.activation(out=res[:, e], in_=logits[:], func=ACT.Identity, bias=b2_column, scale=1.0)
                    else:
                        nc.vector.tensor_scalar_add(out=res[:, e], in0=logits[:], scalar1=b2_column)
                    if (e + 1) % (K_RUN // pieces) == 0:
                        ready = slice(e + 1 - K_RUN // pieces, e + 1)
                        nc.sync.dma_start(
                            out=out_view[g, :, b, IMAGE * ready.start : IMAGE * ready.stop],
                            in_=res[:, ready].rearrange("p e x -> p (e x)"),
                        )
